import numpy as np
import ml_dtypes


def mxq(x, axis, fmt="e4m3"):
    dtype, down = {"e4m3": (ml_dtypes.float8_e4m3fn, 7), "e5m2": (ml_dtypes.float8_e5m2, 14)}[fmt]
    v = np.moveaxis(np.asarray(x, np.float32).astype(ml_dtypes.bfloat16).astype(np.float64), axis, -1)
    blocks = v.reshape(v.shape[:-1] + (-1, 32))
    amax = np.abs(blocks).max(-1, keepdims=True)
    byte = np.maximum(np.where(amax > 0, np.frexp(amax)[1] - 1 + 127, 0) - down, 1)
    scale = np.exp2(byte - 127.0)
    codes = (blocks / scale).astype(np.float32).astype(dtype).astype(np.float64)
    return np.moveaxis((codes * scale).reshape(v.shape), -1, axis)


WIDE = False


def mx_kscale(k):
    if not WIDE:
        return np.ones(k)
    levels = np.array([10, -10, 5, -5, 0])
    a = np.random.permutation(np.resize(levels, k // 512 * 4)).reshape(k // 512, 4)
    idx = np.arange(k)
    return np.exp2(a[idx // 512, idx % 128 // 32])


BF16 = ml_dtypes.bfloat16


def bf(x):
    return np.asarray(x, np.float32).astype(BF16)


def f64(x):
    return np.asarray(x).astype(np.float64)


E2M1 = np.array([0.0, 0.5, 1.0, 1.5, 2.0, 3.0, 4.0, 6.0, -0.0, -0.5, -1.0, -1.5, -2.0, -3.0, -4.0, -6.0])


def pack_weight(w, fmt):
    k, n = w.shape
    w = f64(bf(w)).reshape(k // 32, 32, n)
    amax = np.abs(w).max(1)
    if fmt == "e4m3":
        byte = np.frexp(amax)[1] - 1 + 127 - 7
    else:
        mant, ex = np.frexp(amax / 6.0)
        byte = np.where(mant > 0.5, ex, ex - 1) + 127
    byte = np.clip(np.where(amax > 0, byte, 1), 1, 254)
    scaled = (w * np.exp2(127.0 - byte)[:, None, :]).reshape(k, n).astype(np.float32)
    by_word = np.ascontiguousarray(scaled.reshape(k // 512, 128, 4, n).transpose(0, 1, 3, 2))
    if fmt == "e4m3":
        words = by_word.astype(ml_dtypes.float8_e4m3fn).view(np.uint8)
    else:
        c = by_word.astype(ml_dtypes.float4_e2m1fn).view(np.uint8) & 0xF
        words = c[..., 0::2] | (c[..., 1::2] << 4)
    return np.ascontiguousarray(words), np.ascontiguousarray(byte.astype(np.uint8).reshape(k // 512, 16, n))


def unpack_weight(words, scales, fmt):
    g, p, n, _ = words.shape
    if fmt == "e4m3":
        vals = np.ascontiguousarray(words).view(ml_dtypes.float8_e4m3fn).astype(np.float64)
    else:
        nib = np.empty((g, p, n, 4), np.uint8)
        nib[..., 0::2] = words & 0xF
        nib[..., 1::2] = words >> 4
        vals = E2M1[nib]
    vals = vals * np.repeat(np.exp2(scales.astype(np.float64) - 127.0), 8, axis=1)[..., None]
    return vals.transpose(0, 1, 3, 2).reshape(g * 512, n)


B, S, D, E = 2, 512, 512, 512
EPS = 1e-5
FMT = "e4m3"


def layer_norm(x, g, b):
    mu = x.mean(-1, keepdims=True)
    var = np.square(x - mu).mean(-1, keepdims=True)
    return (x - mu) / np.sqrt(var + EPS) * g + b


def setup_inputs():
    s = mx_kscale(D)

    def stream():
        return bf(np.random.standard_normal((B, S, D)) + 0.5 * np.random.standard_normal((B, S, 1)))

    def gain():
        return bf((1.0 + 0.1 * np.random.standard_normal(D)) * s)

    def shift():
        return bf(0.1 * np.random.standard_normal(D) * s)

    def weight(a):
        w = np.random.standard_normal((E, D)) * a / np.sqrt(D) / s[None, :]
        return pack_weight(np.ascontiguousarray(w.T), FMT)

    def bias():
        return bf(0.2 * np.random.standard_normal(E))

    text = stream()
    img = stream()
    ln_t_g = gain()
    ln_t_b = shift()
    ln_i_g = gain()
    ln_i_b = shift()
    Wq_words, Wq_scales = weight(1.5)
    bq = bias()
    Wkt_words, Wkt_scales = weight(1.5)
    bkt = bias()
    Wvt_words, Wvt_scales = weight(1.0)
    bvt = bias()
    Wki_words, Wki_scales = weight(1.5)
    bki = bias()
    Wvi_words, Wvi_scales = weight(1.0)
    bvi = bias()
    return {"text": text, "img": img,
            "ln_t_g": ln_t_g, "ln_t_b": ln_t_b, "ln_i_g": ln_i_g, "ln_i_b": ln_i_b,
            "Wq_words": Wq_words, "Wq_scales": Wq_scales, "bq": bq,
            "Wkt_words": Wkt_words, "Wkt_scales": Wkt_scales, "bkt": bkt,
            "Wvt_words": Wvt_words, "Wvt_scales": Wvt_scales, "bvt": bvt,
            "Wki_words": Wki_words, "Wki_scales": Wki_scales, "bki": bki,
            "Wvi_words": Wvi_words, "Wvi_scales": Wvi_scales, "bvi": bvi}


def reference(text, img, ln_t_g, ln_t_b, ln_i_g, ln_i_b, Wq_words, Wq_scales, bq, Wkt_words, Wkt_scales, bkt, Wvt_words, Wvt_scales, bvt, Wki_words, Wki_scales, bki, Wvi_words, Wvi_scales, bvi):
    tn = mxq(layer_norm(f64(text), f64(ln_t_g), f64(ln_t_b)), 2, "e4m3")
    im = mxq(layer_norm(f64(img), f64(ln_i_g), f64(ln_i_b)), 2, "e4m3")
    wq = unpack_weight(Wq_words, Wq_scales, FMT)
    q = np.concatenate([(tn @ wq), (im @ wq)], 0) + f64(bq)
    k = np.concatenate([(tn @ unpack_weight(Wkt_words, Wkt_scales, FMT)) + f64(bkt), (im @ unpack_weight(Wki_words, Wki_scales, FMT)) + f64(bki)], 0)
    v = np.concatenate([(tn @ unpack_weight(Wvt_words, Wvt_scales, FMT)) + f64(bvt), (im @ unpack_weight(Wvi_words, Wvi_scales, FMT)) + f64(bvi)], 0)
    return q, k, v

@@ -1,0 +1,276 @@
+from contextlib import ExitStack
+
+import concourse.mybir as mybir
+from concourse.masks import make_identity
+
+F32 = mybir.dt.float32
+BF16 = mybir.dt.bfloat16
+I32 = mybir.dt.int32
+U32 = mybir.dt.uint32
+U8 = mybir.dt.uint8
+FP8X4 = mybir.dt.float8_e4m3fn_x4
+ACT = mybir.ActivationFunctionType
+ALU = mybir.AluOpType
+
+P = 128
+PACK = 4
+K = P * PACK
+N_OUT = 512
+EPS = 1e-5
+
+BLOCK_ROWS = 512
+ROWS_PER_PARTITION = BLOCK_ROWS // P
+N_BLOCKS = 4
+BLOCKS_PER_STREAM = 2
+UNIT_J = 2
+UNITS_PER_BLOCK = ROWS_PER_PARTITION // UNIT_J
+UNIT_ROWS = UNIT_J * P
+N_UNITS = N_BLOCKS * UNITS_PER_BLOCK
+UNITS_PER_STREAM = BLOCKS_PER_STREAM * UNITS_PER_BLOCK
+
+N_WEIGHTS = 5
+WEIGHTS_USED_BY = ((0, 1, 2), (0, 3, 4))
+WEIGHTS_FIRST_USED_BY = ((0, 1, 2), (3, 4))
+SCALE_ROWS = K // 32
+QUADRANT = 32
+
+BN_STATS_DIM = 6
+BN_AGGR_DIM = 2
+VECTOR_PAD = 16
+
+STATS_AHEAD = 6
+
+FLOPS = 2 * N_BLOCKS * BLOCK_ROWS * K * 3 * N_OUT
+
+
+def tile_modalityadaptivemodule_pa_kernel(
+    tc,
+    text, img, ln_t_g, ln_t_b, ln_i_g, ln_i_b,
+    Wq_words, Wq_scales, bq,
+    Wkt_words, Wkt_scales, bkt,
+    Wvt_words, Wvt_scales, bvt,
+    Wki_words, Wki_scales, bki,
+    Wvi_words, Wvi_scales, bvi,
+    out_0, out_1, out_2,
+):
+    nc = tc.nc
+    streams = (text, img)
+    gains_shifts = ((ln_t_g, ln_t_b), (ln_i_g, ln_i_b))
+    weight_words = (Wq_words, Wkt_words, Wvt_words, Wki_words, Wvi_words)
+    weight_scales = (Wq_scales, Wkt_scales, Wvt_scales, Wki_scales, Wvi_scales)
+    biases = (bq, bkt, bvt, bki, bvi)
+    outs = (out_0, out_1, out_2)
+
+    with ExitStack() as ctx:
+        keep = ctx.enter_context(tc.tile_pool(name="keep", bufs=1))
+        xhat_pool = ctx.enter_context(tc.tile_pool(name="xhat_pool", bufs=3))
+        tn_pool = ctx.enter_context(tc.tile_pool(name="tn_pool", bufs=2))
+        operand_pool = ctx.enter_context(tc.tile_pool(name="operand_pool", bufs=3))
+        result_pool = ctx.enter_context(tc.tile_pool(name="result_pool", bufs=8))
+        xt_psum = ctx.enter_context(tc.psum_pool(name="xt_psum", bufs=2))
+        acc_psum = ctx.enter_context(tc.psum_pool(name="acc_psum", bufs=4))
+        ctx.enter_context(tc.manual_schedule())
+
+        x_sb = [
+            keep.tile([P, ROWS_PER_PARTITION, K], BF16, name="x%d" % b)
+            for b in range(N_BLOCKS)
+        ]
+        w_words = keep.tile([P, N_WEIGHTS, N_OUT], U32, align_bytes=64)
+        w_scales = keep.tile([P, N_WEIGHTS, N_OUT], U8, align_bytes=64)
+        gain_shift_bf = keep.tile([P, 2, 2, VECTOR_PAD], BF16)
+        gain_shift = keep.tile([P, 2, 2, PACK], F32)
+        bias_rows = keep.tile([P, N_WEIGHTS, N_OUT], BF16)
+        bias_all = keep.tile([P, N_WEIGHTS, N_OUT], F32)
+        ones = keep.tile([P, P], BF16)
+        ident = keep.tile([P, P], F32)
+        neg_half = keep.tile([P, UNIT_J], F32)
+        stats = keep.tile([P, N_UNITS, UNIT_J, BN_STATS_DIM], F32)
+        mean_var = keep.tile([P, N_UNITS, UNIT_J, BN_AGGR_DIM], F32)
+        neg_mean = keep.tile([P, N_UNITS, UNIT_J], F32)
+        var_eps = keep.tile([P, N_UNITS, UNIT_J], F32)
+        rstd = keep.tile([P, N_UNITS, UNIT_J], F32)
+
+        xhat_of = {}
+        xt_of = {}
+        grouped_of = {}
+        operand_of = {}
+
+        def block_view(dram, b):
+            return dram[b].rearrange("(p j) c -> p j c", j=ROWS_PER_PARTITION)
+
+        def unit_place(u):
+            b, half = divmod(u, UNITS_PER_BLOCK)
+            return b, half * UNIT_J
+
+        def load_rows(b, j0, j1):
+            source = block_view(streams[b // BLOCKS_PER_STREAM], b % BLOCKS_PER_STREAM)
+            nc.sync.dma_start(out=x_sb[b][:, j0:j1, :], in_=source[:, j0:j1, :])
+
+        def load_vectors(s):
+            with nc.allow_non_contiguous_dma(reason="four bfloat16 values to a partition"):
+                for i in range(2):
+                    nc.sync.dma_start(
+                        out=gain_shift_bf[:, s, i, 0:PACK],
+                        in_=gains_shifts[s][i].rearrange("(p t) -> p t", t=PACK),
+                    )
+            for w in WEIGHTS_FIRST_USED_BY[s]:
+                nc.sync.dma_start(
+                    out=bias_rows[0:1, w, :], in_=biases[w].rearrange("(o n) -> o n", o=1)
+                )
+
+        def load_weight(w):
+            for quad in range(SCALE_ROWS // PACK):
+                nc.sync.dma_start(
+                    out=w_scales[QUADRANT * quad : QUADRANT * quad + PACK, w, :].bitcast(I32),
+                    in_=weight_scales[w][0, PACK * quad : PACK * (quad + 1), :].bitcast(I32),
+                )
+            nc.sync.dma_start(
+                out=w_words[:, w, :].bitcast(I32),
+                in_=weight_words[w][0].rearrange("p n t -> p (n t)").bitcast(I32),
+            )
+
+        nc.vector.memset(w_scales[:].bitcast(I32), 0)
+        nc.vector.memset(bias_rows[:], 0.0)
+        nc.vector.memset(ones[:], 1.0)
+        nc.gpsimd.memset(neg_half[:], -0.5)
+        make_identity(nc, ident[:])
+
+        load_rows(0, 0, UNIT_J)
+        load_rows(0, UNIT_J, ROWS_PER_PARTITION)
+        load_vectors(0)
+        load_rows(1, 0, ROWS_PER_PARTITION)
+        load_rows(2, 0, ROWS_PER_PARTITION)
+        for w in WEIGHTS_FIRST_USED_BY[0]:
+            load_weight(w)
+        load_rows(3, 0, ROWS_PER_PARTITION)
+        load_vectors(1)
+        for w in WEIGHTS_FIRST_USED_BY[1]:
+            load_weight(w)
+
+        def prepare_stream(s):
+            nc.scalar.activation(
+                out=gain_shift[:, s, :, :], in_=gain_shift_bf[:, s, :, 0:PACK], func=ACT.Identity
+            )
+            for w in WEIGHTS_FIRST_USED_BY[s]:
+                acc = acc_psum.tile([P, N_OUT], F32)
+                nc.tensor.matmul(
+                    out=acc[:], lhsT=ones[:], rhs=bias_rows[:, w, :], start=True, stop=True
+                )
+                nc.scalar.copy(out=bias_all[:, w, :], in_=acc[:])
+
+        def statistics(u):
+            b, j0 = unit_place(u)
+            for jj in range(UNIT_J):
+                nc.vector.bn_stats(out=stats[:, u, jj, :], in_=x_sb[b][:, j0 + jj, :])
+            for jj in range(UNIT_J):
+                nc.vector.bn_aggr(out=mean_var[:, u, jj, :], in_=stats[:, u, jj, :])
+
+        def normalise(u):
+            b, j0 = unit_place(u)
+            nc.gpsimd.tensor_scalar(
+                out=neg_mean[:, u, :], in0=mean_var[:, u, :, 0],
+                scalar1=-1.0, scalar2=0.0, op0=ALU.mult, op1=ALU.add,
+            )
+            nc.gpsimd.tensor_scalar(
+                out=var_eps[:, u, :], in0=mean_var[:, u, :, 1],
+                scalar1=1.0, scalar2=EPS, op0=ALU.mult, op1=ALU.add,
+            )
+            nc.gpsimd.tensor_tensor(
+                out=rstd[:, u, :], in0=var_eps[:, u, :], in1=neg_half[:], op=ALU.pow
+            )
+            xhat = xhat_pool.tile([P, UNIT_J, PACK, P], F32)
+            for jj in range(UNIT_J):
+                nc.gpsimd.tensor_scalar(
+                    out=xhat[:, jj, :, :],
+                    in0=x_sb[b][:, j0 + jj, :].rearrange("p (q t) -> p t q", t=PACK),
+                    scalar1=neg_mean[:, u, jj : jj + 1], scalar2=rstd[:, u, jj : jj + 1],
+                    op0=ALU.add, op1=ALU.mult,
+                )
+            xhat_of[u] = xhat
+
+        def transpose(u):
+            xhat = xhat_of[u]
+            xt_lo = xt_psum.tile([P, 2, UNIT_ROWS], F32)
+            xt_hi = xt_psum.tile([P, 2, UNIT_ROWS], F32)
+            xt_of[u] = [xt_lo[:, 0, :], xt_lo[:, 1, :], xt_hi[:, 0, :], xt_hi[:, 1, :]]
+            for jj in range(UNIT_J):
+                for t in range(PACK):
+                    nc.tensor.transpose(
+                        out=xt_of[u][t][:, jj * P : (jj + 1) * P],
+                        in_=xhat[:, jj, t, :],
+                        identity=ident[:],
+                    )
+
+        def scale_shift(u):
+            s = u // UNITS_PER_STREAM
+            planes = tn_pool.tile([P, PACK, UNIT_ROWS], BF16)
+            for t in range(PACK):
+                nc.scalar.activation(
+                    out=planes[:, t, :], in_=xt_of[u][t], func=ACT.Identity,
+                    scale=gain_shift[:, s, 0, t : t + 1], bias=gain_shift[:, s, 1, t : t + 1],
+                )
+            grouped = tn_pool.tile([P, UNIT_ROWS, PACK], BF16, align_bytes=64)
+            nc.scalar.copy(
+                out=grouped[:].rearrange("p (c i) t -> p c t i", i=4),
+                in_=planes[:].rearrange("p t (c i) -> p c t i", i=4),
+            )
+            grouped_of[u] = grouped
+
+        def quantise(u):
+            codes = operand_pool.tile([P, UNIT_ROWS], U32, align_bytes=64)
+            code_scales = operand_pool.tile([P, UNIT_ROWS], U8, align_bytes=64)
+            nc.vector.quantize_mx(
+                out=codes[:].bitcast(FP8X4),
+                scales=code_scales[:],
+                in_=grouped_of[u][:].rearrange("p c t -> p (c t)"),
+            )
+            operand_of[u] = (codes, code_scales)
+
+        def project(u, o):
+            b, j0 = unit_place(u)
+            w = WEIGHTS_USED_BY[u // UNITS_PER_STREAM][o]
+            codes, code_scales = operand_of[u]
+            result = result_pool.tile([P, UNIT_J, N_OUT], F32)
+            for jj in range(UNIT_J):
+                rows = slice(jj * P, (jj + 1) * P)
+                acc = acc_psum.tile([P, N_OUT], F32)
+                nc.tensor.matmul_mx(
+                    out=acc[:],
+                    lhsT=codes[:, rows].bitcast(FP8X4),
+                    lhsT_scale=code_scales[:, rows],
+                    rhs=w_words[:, w, :].bitcast(FP8X4),
+                    rhs_scale=w_scales[:, w, :],
+                    start=True,
+                    stop=True,
+                )
+                nc.vector.tensor_tensor(
+                    out=result[:, jj, :], in0=acc[:], in1=bias_all[:, w, :], op=ALU.add
+                )
+            nc.sync.dma_start(
+                out=block_view(outs[o], b)[:, j0 : j0 + UNIT_J, :], in_=result[:]
+            )
+
+        for u in range(STATS_AHEAD):
+            statistics(u)
+        prepare_stream(0)
+        normalise(0)
+        transpose(0)
+        normalise(1)
+        transpose(1)
+        scale_shift(0)
+        quantise(0)
+        for u in range(N_UNITS):
+            if u + 1 < N_UNITS:
+                scale_shift(u + 1)
+            project(u, 0)
+            project(u, 1)
+            if u + 1 < N_UNITS:
+                quantise(u + 1)
+            project(u, 2)
+            if u + STATS_AHEAD < N_UNITS:
+                statistics(u + STATS_AHEAD)
+            if u + 2 < N_UNITS:
+                if (u + 2) % UNITS_PER_STREAM == 0:
+                    prepare_stream((u + 2) // UNITS_PER_STREAM)
+                normalise(u + 2)
+                transpose(u + 2)

@@ -38,7 +38,8 @@ BN_STATS_DIM = 6
 BN_AGGR_DIM = 2
 VECTOR_PAD = 16
 
-STATS_AHEAD = 6
+VECTOR_STATS_UNITS = 6
+SCALAR_STATS_UNITS = N_UNITS - VECTOR_STATS_UNITS
 
 FLOPS = 2 * N_BLOCKS * BLOCK_ROWS * K * 3 * N_OUT
 
@@ -67,6 +68,7 @@ def tile_modalityadaptivemodule_pa_kernel(
         tn_pool = ctx.enter_context(tc.tile_pool(name="tn_pool", bufs=2))
         operand_pool = ctx.enter_context(tc.tile_pool(name="operand_pool", bufs=3))
         result_pool = ctx.enter_context(tc.tile_pool(name="result_pool", bufs=8))
+        unread_pool = ctx.enter_context(tc.tile_pool(name="unread_pool", bufs=4))
         xt_psum = ctx.enter_context(tc.psum_pool(name="xt_psum", bufs=2))
         acc_psum = ctx.enter_context(tc.psum_pool(name="acc_psum", bufs=4))
         ctx.enter_context(tc.manual_schedule())
@@ -84,9 +86,11 @@ def tile_modalityadaptivemodule_pa_kernel(
         ones = keep.tile([P, P], BF16)
         ident = keep.tile([P, P], F32)
         neg_half = keep.tile([P, UNIT_J], F32)
-        stats = keep.tile([P, N_UNITS, UNIT_J, BN_STATS_DIM], F32)
-        mean_var = keep.tile([P, N_UNITS, UNIT_J, BN_AGGR_DIM], F32)
-        neg_mean = keep.tile([P, N_UNITS, UNIT_J], F32)
+        stats = keep.tile([P, VECTOR_STATS_UNITS, UNIT_J, BN_STATS_DIM], F32)
+        mean_var = keep.tile([P, VECTOR_STATS_UNITS, UNIT_J, BN_AGGR_DIM], F32)
+        neg_mean = keep.tile([P, VECTOR_STATS_UNITS, UNIT_J], F32)
+        neg_mean_scalar = keep.tile([P, SCALAR_STATS_UNITS, UNIT_J], F32)
+        sum_squares = keep.tile([P, SCALAR_STATS_UNITS, UNIT_J], F32)
         var_eps = keep.tile([P, N_UNITS, UNIT_J], F32)
         rstd = keep.tile([P, N_UNITS, UNIT_J], F32)
 
@@ -165,16 +169,38 @@ def tile_modalityadaptivemodule_pa_kernel(
             for jj in range(UNIT_J):
                 nc.vector.bn_aggr(out=mean_var[:, u, jj, :], in_=stats[:, u, jj, :])
 
+        def statistics_on_scalar(u, jj):
+            b, j0 = unit_place(u)
+            i = u - VECTOR_STATS_UNITS
+            scaled = unread_pool.tile([P, K], BF16)
+            nc.scalar.activation(
+                out=scaled[:], in_=x_sb[b][:, j0 + jj, :], func=ACT.Identity,
+                scale=-1.0 / K, accum_out=neg_mean_scalar[:, i, jj : jj + 1],
+            )
+            squares = unread_pool.tile([P, K], BF16)
+            nc.scalar.activation(
+                out=squares[:], in_=x_sb[b][:, j0 + jj, :], func=ACT.Square,
+                bias=neg_mean_scalar[:, i, jj : jj + 1], accum_out=sum_squares[:, i, jj : jj + 1],
+            )
+
         def normalise(u):
             b, j0 = unit_place(u)
-            nc.gpsimd.tensor_scalar(
-                out=neg_mean[:, u, :], in0=mean_var[:, u, :, 0],
-                scalar1=-1.0, scalar2=0.0, op0=ALU.mult, op1=ALU.add,
-            )
-            nc.gpsimd.tensor_scalar(
-                out=var_eps[:, u, :], in0=mean_var[:, u, :, 1],
-                scalar1=1.0, scalar2=EPS, op0=ALU.mult, op1=ALU.add,
-            )
+            if u < VECTOR_STATS_UNITS:
+                unit_neg_mean = neg_mean[:, u, :]
+                nc.gpsimd.tensor_scalar(
+                    out=unit_neg_mean, in0=mean_var[:, u, :, 0],
+                    scalar1=-1.0, scalar2=0.0, op0=ALU.mult, op1=ALU.add,
+                )
+                nc.gpsimd.tensor_scalar(
+                    out=var_eps[:, u, :], in0=mean_var[:, u, :, 1],
+                    scalar1=1.0, scalar2=EPS, op0=ALU.mult, op1=ALU.add,
+                )
+            else:
+                unit_neg_mean = neg_mean_scalar[:, u - VECTOR_STATS_UNITS, :]
+                nc.gpsimd.tensor_scalar(
+                    out=var_eps[:, u, :], in0=sum_squares[:, u - VECTOR_STATS_UNITS, :],
+                    scalar1=1.0 / K, scalar2=EPS, op0=ALU.mult, op1=ALU.add,
+                )
             nc.gpsimd.tensor_tensor(
                 out=rstd[:, u, :], in0=var_eps[:, u, :], in1=neg_half[:], op=ALU.pow
             )
@@ -183,7 +209,7 @@ def tile_modalityadaptivemodule_pa_kernel(
                 nc.gpsimd.tensor_scalar(
                     out=xhat[:, jj, :, :],
                     in0=x_sb[b][:, j0 + jj, :].rearrange("p (q t) -> p t q", t=PACK),
-                    scalar1=neg_mean[:, u, jj : jj + 1], scalar2=rstd[:, u, jj : jj + 1],
+                    scalar1=unit_neg_mean[:, jj : jj + 1], scalar2=rstd[:, u, jj : jj + 1],
                     op0=ALU.add, op1=ALU.mult,
                 )
             xhat_of[u] = xhat
@@ -250,7 +276,7 @@ def tile_modalityadaptivemodule_pa_kernel(
                 out=block_view(outs[o], b)[:, j0 : j0 + UNIT_J, :], in_=result[:]
             )
 
-        for u in range(STATS_AHEAD):
+        for u in range(VECTOR_STATS_UNITS):
             statistics(u)
         prepare_stream(0)
         normalise(0)
@@ -262,13 +288,13 @@ def tile_modalityadaptivemodule_pa_kernel(
         for u in range(N_UNITS):
             if u + 1 < N_UNITS:
                 scale_shift(u + 1)
+            if u < SCALAR_STATS_UNITS * UNIT_J:
+                statistics_on_scalar(VECTOR_STATS_UNITS + u // UNIT_J, u % UNIT_J)
             project(u, 0)
             project(u, 1)
             if u + 1 < N_UNITS:
                 quantise(u + 1)
             project(u, 2)
-            if u + STATS_AHEAD < N_UNITS:
-                statistics(u + STATS_AHEAD)
             if u + 2 < N_UNITS:
                 if (u + 2) % UNITS_PER_STREAM == 0:
                     prepare_stream((u + 2) // UNITS_PER_STREAM)

@@ -34,6 +34,8 @@ WEIGHTS_FIRST_USED_BY = ((0, 1, 2), (3, 4))
 SCALE_ROWS = K // 32
 QUADRANT = 32
 
+SELECT_COLUMNS = 16
+
 BN_STATS_DIM = 6
 BN_AGGR_DIM = 2
 VECTOR_PAD = 16
@@ -81,10 +83,10 @@ def tile_modalityadaptivemodule_pa_kernel(
         w_scales = keep.tile([P, N_WEIGHTS, N_OUT], U8, align_bytes=64)
         gain_shift_bf = keep.tile([P, 2, 2, VECTOR_PAD], BF16)
         gain_shift = keep.tile([P, 2, 2, PACK], F32)
-        bias_rows = keep.tile([P, N_WEIGHTS, N_OUT], BF16)
+        bias_rows = keep.tile([P, N_OUT], BF16)
         bias_all = keep.tile([P, N_WEIGHTS, N_OUT], F32)
-        ones = keep.tile([P, P], BF16)
         ident = keep.tile([P, P], F32)
+        select = keep.tile([P, SELECT_COLUMNS], BF16)
         neg_half = keep.tile([P, UNIT_J], F32)
         stats = keep.tile([P, VECTOR_STATS_UNITS, UNIT_J, BN_STATS_DIM], F32)
         mean_var = keep.tile([P, VECTOR_STATS_UNITS, UNIT_J, BN_AGGR_DIM], F32)
@@ -110,6 +112,12 @@ def tile_modalityadaptivemodule_pa_kernel(
             source = block_view(streams[b // BLOCKS_PER_STREAM], b % BLOCKS_PER_STREAM)
             nc.sync.dma_start(out=x_sb[b][:, j0:j1, :], in_=source[:, j0:j1, :])
 
+        def load_biases():
+            for w in range(N_WEIGHTS):
+                nc.sync.dma_start(
+                    out=bias_rows[w : w + 1, :], in_=biases[w].rearrange("(o n) -> o n", o=1)
+                )
+
         def load_vectors(s):
             with nc.allow_non_contiguous_dma(reason="four bfloat16 values to a partition"):
                 for i in range(2):
@@ -117,39 +125,42 @@ def tile_modalityadaptivemodule_pa_kernel(
                         out=gain_shift_bf[:, s, i, 0:PACK],
                         in_=gains_shifts[s][i].rearrange("(p t) -> p t", t=PACK),
                     )
-            for w in WEIGHTS_FIRST_USED_BY[s]:
-                nc.sync.dma_start(
-                    out=bias_rows[0:1, w, :], in_=biases[w].rearrange("(o n) -> o n", o=1)
-                )
 
-        def load_weight(w):
+        def load_scales(w):
             for quad in range(SCALE_ROWS // PACK):
                 nc.sync.dma_start(
                     out=w_scales[QUADRANT * quad : QUADRANT * quad + PACK, w, :].bitcast(I32),
                     in_=weight_scales[w][0, PACK * quad : PACK * (quad + 1), :].bitcast(I32),
                 )
+
+        def load_words(w):
             nc.sync.dma_start(
                 out=w_words[:, w, :].bitcast(I32),
                 in_=weight_words[w][0].rearrange("p n t -> p (n t)").bitcast(I32),
             )
 
-        nc.vector.memset(w_scales[:].bitcast(I32), 0)
-        nc.vector.memset(bias_rows[:], 0.0)
-        nc.vector.memset(ones[:], 1.0)
-        nc.gpsimd.memset(neg_half[:], -0.5)
+        nc.gpsimd.memset(bias_rows[:].bitcast(I32), 0)
+        nc.gpsimd.memset(w_scales[:].bitcast(I32), 0)
         make_identity(nc, ident[:])
+        nc.gpsimd.tensor_copy(out=select[:], in_=ident[:, 0:SELECT_COLUMNS])
+        nc.gpsimd.memset(neg_half[:], -0.5)
 
         load_rows(0, 0, UNIT_J)
         load_rows(0, UNIT_J, ROWS_PER_PARTITION)
+        load_biases()
         load_vectors(0)
         load_rows(1, 0, ROWS_PER_PARTITION)
         load_rows(2, 0, ROWS_PER_PARTITION)
         for w in WEIGHTS_FIRST_USED_BY[0]:
-            load_weight(w)
+            load_scales(w)
+        for w in WEIGHTS_FIRST_USED_BY[0]:
+            load_words(w)
         load_rows(3, 0, ROWS_PER_PARTITION)
         load_vectors(1)
         for w in WEIGHTS_FIRST_USED_BY[1]:
-            load_weight(w)
+            load_scales(w)
+        for w in WEIGHTS_FIRST_USED_BY[1]:
+            load_words(w)
 
         def prepare_stream(s):
             nc.scalar.activation(
@@ -158,7 +169,8 @@ def tile_modalityadaptivemodule_pa_kernel(
             for w in WEIGHTS_FIRST_USED_BY[s]:
                 acc = acc_psum.tile([P, N_OUT], F32)
                 nc.tensor.matmul(
-                    out=acc[:], lhsT=ones[:], rhs=bias_rows[:, w, :], start=True, stop=True
+                    out=acc[:], lhsT=select[:, w : w + 1].to_broadcast([P, P]), rhs=bias_rows[:],
+                    start=True, stop=True,
                 )
                 nc.scalar.copy(out=bias_all[:, w, :], in_=acc[:])
 

@@ -42,6 +42,7 @@ VECTOR_PAD = 16
 
 VECTOR_STATS_UNITS = 6
 SCALAR_STATS_UNITS = N_UNITS - VECTOR_STATS_UNITS
+FIRST_STATS_UNITS = 4
 
 FLOPS = 2 * N_BLOCKS * BLOCK_ROWS * K * 3 * N_OUT
 
@@ -66,7 +67,7 @@ def tile_modalityadaptivemodule_pa_kernel(
 
     with ExitStack() as ctx:
         keep = ctx.enter_context(tc.tile_pool(name="keep", bufs=1))
-        xhat_pool = ctx.enter_context(tc.tile_pool(name="xhat_pool", bufs=3))
+        xhat_pool = ctx.enter_context(tc.tile_pool(name="xhat_pool", bufs=N_UNITS))
         tn_pool = ctx.enter_context(tc.tile_pool(name="tn_pool", bufs=2))
         operand_pool = ctx.enter_context(tc.tile_pool(name="operand_pool", bufs=3))
         result_pool = ctx.enter_context(tc.tile_pool(name="result_pool", bufs=8))
@@ -86,14 +87,14 @@ def tile_modalityadaptivemodule_pa_kernel(
         bias_rows = keep.tile([P, N_OUT], BF16)
         bias_all = keep.tile([P, N_WEIGHTS, N_OUT], F32)
         ident = keep.tile([P, P], F32)
+        std = keep.tile([P, N_UNITS, UNIT_J], F32)
+        one = keep.tile([P, 1], F32)
+        unread_root = keep.tile([P, 1], F32)
         select = keep.tile([P, SELECT_COLUMNS], BF16)
-        neg_half = keep.tile([P, UNIT_J], F32)
         stats = keep.tile([P, VECTOR_STATS_UNITS, UNIT_J, BN_STATS_DIM], F32)
         mean_var = keep.tile([P, VECTOR_STATS_UNITS, UNIT_J, BN_AGGR_DIM], F32)
-        neg_mean = keep.tile([P, VECTOR_STATS_UNITS, UNIT_J], F32)
-        neg_mean_scalar = keep.tile([P, SCALAR_STATS_UNITS, UNIT_J], F32)
-        sum_squares = keep.tile([P, SCALAR_STATS_UNITS, UNIT_J], F32)
-        var_eps = keep.tile([P, N_UNITS, UNIT_J], F32)
+        neg_mean = keep.tile([P, N_UNITS, UNIT_J], F32)
+        sum_squares = keep.tile([P, N_UNITS, UNIT_J], F32)
         rstd = keep.tile([P, N_UNITS, UNIT_J], F32)
 
         xhat_of = {}
@@ -139,11 +140,13 @@ def tile_modalityadaptivemodule_pa_kernel(
                 in_=weight_words[w][0].rearrange("p n t -> p (n t)").bitcast(I32),
             )
 
+        nc.gpsimd.memset(one[:], 1.0)
         nc.gpsimd.memset(bias_rows[:].bitcast(I32), 0)
         nc.gpsimd.memset(w_scales[:].bitcast(I32), 0)
         make_identity(nc, ident[:])
         nc.gpsimd.tensor_copy(out=select[:], in_=ident[:, 0:SELECT_COLUMNS])
-        nc.gpsimd.memset(neg_half[:], -0.5)
+
+        nc.scalar.activation(out=unread_root[:], in_=one[:], func=ACT.Sqrt)
 
         load_rows(0, 0, UNIT_J)
         load_rows(0, UNIT_J, ROWS_PER_PARTITION)
@@ -157,15 +160,9 @@ def tile_modalityadaptivemodule_pa_kernel(
             load_words(w)
         load_rows(3, 0, ROWS_PER_PARTITION)
         load_vectors(1)
-        for w in WEIGHTS_FIRST_USED_BY[1]:
-            load_scales(w)
-        for w in WEIGHTS_FIRST_USED_BY[1]:
-            load_words(w)
 
         def prepare_stream(s):
-            nc.scalar.activation(
-                out=gain_shift[:, s, :, :], in_=gain_shift_bf[:, s, :, 0:PACK], func=ACT.Identity
-            )
+            nc.scalar.copy(out=gain_shift[:, s, :, :], in_=gain_shift_bf[:, s, :, 0:PACK])
             for w in WEIGHTS_FIRST_USED_BY[s]:
                 acc = acc_psum.tile([P, N_OUT], F32)
                 nc.tensor.matmul(
@@ -183,45 +180,40 @@ def tile_modalityadaptivemodule_pa_kernel(
 
         def statistics_on_scalar(u, jj):
             b, j0 = unit_place(u)
-            i = u - VECTOR_STATS_UNITS
             scaled = unread_pool.tile([P, K], BF16)
             nc.scalar.activation(
                 out=scaled[:], in_=x_sb[b][:, j0 + jj, :], func=ACT.Identity,
-                scale=-1.0 / K, accum_out=neg_mean_scalar[:, i, jj : jj + 1],
+                scale=-1.0 / K, accum_out=neg_mean[:, u, jj : jj + 1],
             )
             squares = unread_pool.tile([P, K], BF16)
             nc.scalar.activation(
                 out=squares[:], in_=x_sb[b][:, j0 + jj, :], func=ACT.Square,
-                bias=neg_mean_scalar[:, i, jj : jj + 1], accum_out=sum_squares[:, i, jj : jj + 1],
+                bias=neg_mean[:, u, jj : jj + 1], accum_out=sum_squares[:, u, jj : jj + 1],
             )
 
-        def normalise(u):
-            b, j0 = unit_place(u)
+        def deviation(u):
             if u < VECTOR_STATS_UNITS:
-                unit_neg_mean = neg_mean[:, u, :]
-                nc.gpsimd.tensor_scalar(
-                    out=unit_neg_mean, in0=mean_var[:, u, :, 0],
-                    scalar1=-1.0, scalar2=0.0, op0=ALU.mult, op1=ALU.add,
+                nc.scalar.activation(
+                    out=std[:, u, :], in_=mean_var[:, u, :, 1], func=ACT.Sqrt, bias=EPS
                 )
-                nc.gpsimd.tensor_scalar(
-                    out=var_eps[:, u, :], in0=mean_var[:, u, :, 1],
-                    scalar1=1.0, scalar2=EPS, op0=ALU.mult, op1=ALU.add,
-                )
+                nc.scalar.mul(out=neg_mean[:, u, :], in_=mean_var[:, u, :, 0], mul=-1.0)
             else:
-                unit_neg_mean = neg_mean_scalar[:, u - VECTOR_STATS_UNITS, :]
-                nc.gpsimd.tensor_scalar(
-                    out=var_eps[:, u, :], in0=sum_squares[:, u - VECTOR_STATS_UNITS, :],
-                    scalar1=1.0 / K, scalar2=EPS, op0=ALU.mult, op1=ALU.add,
+                nc.scalar.activation(
+                    out=std[:, u, :], in_=sum_squares[:, u, :], func=ACT.Sqrt,
+                    scale=1.0 / K, bias=EPS,
                 )
-            nc.gpsimd.tensor_tensor(
-                out=rstd[:, u, :], in0=var_eps[:, u, :], in1=neg_half[:], op=ALU.pow
-            )
+
+        def invert(u):
+            nc.vector.reciprocal(out=rstd[:, u, :], in_=std[:, u, :])
+
+        def normalise(u, engine=nc.gpsimd):
+            b, j0 = unit_place(u)
             xhat = xhat_pool.tile([P, UNIT_J, PACK, P], F32)
             for jj in range(UNIT_J):
-                nc.gpsimd.tensor_scalar(
+                engine.tensor_scalar(
                     out=xhat[:, jj, :, :],
                     in0=x_sb[b][:, j0 + jj, :].rearrange("p (q t) -> p t q", t=PACK),
-                    scalar1=unit_neg_mean[:, jj : jj + 1], scalar2=rstd[:, u, jj : jj + 1],
+                    scalar1=neg_mean[:, u, jj : jj + 1], scalar2=rstd[:, u, jj : jj + 1],
                     op0=ALU.add, op1=ALU.mult,
                 )
             xhat_of[u] = xhat
@@ -238,6 +230,31 @@ def tile_modalityadaptivemodule_pa_kernel(
                         in_=xhat[:, jj, t, :],
                         identity=ident[:],
                     )
+
+        def scale_shift_by_row(u):
+            s = u // UNITS_PER_STREAM
+            planes = tn_pool.tile([P, PACK, UNIT_ROWS], BF16)
+            grouped = tn_pool.tile([P, UNIT_ROWS, PACK], BF16, align_bytes=64)
+            xt_rows = []
+            for jj in range(UNIT_J):
+                xt_lo = xt_psum.tile([P, PACK, P], F32)
+                xt_rows.append(xt_lo)
+                for t in range(PACK):
+                    nc.tensor.transpose(
+                        out=xt_lo[:, t, :], in_=xhat_of[u][:, jj, t, :], identity=ident[:]
+                    )
+            for jj in range(UNIT_J):
+                columns = slice(jj * P, (jj + 1) * P)
+                for t in range(PACK):
+                    nc.scalar.activation(
+                        out=planes[:, t, columns], in_=xt_rows[jj][:, t, :], func=ACT.Identity,
+                        scale=gain_shift[:, s, 0, t : t + 1], bias=gain_shift[:, s, 1, t : t + 1],
+                    )
+            nc.scalar.copy(
+                out=grouped[:].rearrange("p (c i) t -> p c t i", i=4),
+                in_=planes[:].rearrange("p t (c i) -> p c t i", i=4),
+            )
+            grouped_of[u] = grouped
 
         def scale_shift(u):
             s = u // UNITS_PER_STREAM
@@ -288,27 +305,49 @@ def tile_modalityadaptivemodule_pa_kernel(
                 out=block_view(outs[o], b)[:, j0 : j0 + UNIT_J, :], in_=result[:]
             )
 
-        for u in range(VECTOR_STATS_UNITS):
-            statistics(u)
+        statistics(0)
+        deviation(0)
+        invert(0)
+        normalise(0, nc.vector)
+        statistics(1)
         prepare_stream(0)
-        normalise(0)
-        transpose(0)
+        deviation(1)
+        scale_shift_by_row(0)
+        statistics(2)
+        invert(1)
         normalise(1)
-        transpose(1)
-        scale_shift(0)
+        statistics(3)
+        deviation(2)
         quantise(0)
+        invert(2)
+        normalise(2)
         for u in range(N_UNITS):
+            if u == 0:
+                project(0, 0)
+                transpose(1)
             if u + 1 < N_UNITS:
                 scale_shift(u + 1)
+            if u + 3 < N_UNITS:
+                deviation(u + 3)
             if u < SCALAR_STATS_UNITS * UNIT_J:
                 statistics_on_scalar(VECTOR_STATS_UNITS + u // UNIT_J, u % UNIT_J)
-            project(u, 0)
+            if u > 0:
+                project(u, 0)
+            if FIRST_STATS_UNITS + u < VECTOR_STATS_UNITS:
+                statistics(FIRST_STATS_UNITS + u)
             project(u, 1)
+            if u == 0:
+                for w in WEIGHTS_FIRST_USED_BY[1]:
+                    load_scales(w)
+                for w in WEIGHTS_FIRST_USED_BY[1]:
+                    load_words(w)
             if u + 1 < N_UNITS:
                 quantise(u + 1)
+            if u + 3 < N_UNITS:
+                invert(u + 3)
+                normalise(u + 3)
             project(u, 2)
             if u + 2 < N_UNITS:
                 if (u + 2) % UNITS_PER_STREAM == 0:
                     prepare_stream((u + 2) // UNITS_PER_STREAM)
-                normalise(u + 2)
                 transpose(u + 2)

@@ -28,6 +28,7 @@ UNIT_ROWS = UNIT_J * P
 N_UNITS = N_BLOCKS * UNITS_PER_BLOCK
 UNITS_PER_STREAM = BLOCKS_PER_STREAM * UNITS_PER_BLOCK
 
+N_OUTPUTS = 3
 N_WEIGHTS = 5
 WEIGHTS_USED_BY = ((0, 1, 2), (0, 3, 4))
 WEIGHTS_FIRST_USED_BY = ((0, 1, 2), (3, 4))
@@ -40,9 +41,14 @@ BN_STATS_DIM = 6
 BN_AGGR_DIM = 2
 VECTOR_PAD = 16
 
-VECTOR_STATS_UNITS = 6
-SCALAR_STATS_UNITS = N_UNITS - VECTOR_STATS_UNITS
-FIRST_STATS_UNITS = 4
+SCALAR_STATS = (1, 6, 7)
+
+SCALAR_ROWS = (((6, 0),), ((6, 1),), ((7, 0),), ((7, 1),), (), (), (), ())
+VECTOR_UNITS = ((4,), (5,), (), (), (), (), (), ())
+NO_SUMS = ()
+ONE_SUM = ((1, 1),)
+TWO_SUMS = ((1, 1), (2, 1))
+SCALAR_SUMS = (NO_SUMS, NO_SUMS, NO_SUMS, NO_SUMS, NO_SUMS, ONE_SUM, ONE_SUM, ONE_SUM)
 
 FLOPS = 2 * N_BLOCKS * BLOCK_ROWS * K * 3 * N_OUT
 
@@ -72,8 +78,9 @@ def tile_modalityadaptivemodule_pa_kernel(
         operand_pool = ctx.enter_context(tc.tile_pool(name="operand_pool", bufs=3))
         result_pool = ctx.enter_context(tc.tile_pool(name="result_pool", bufs=8))
         unread_pool = ctx.enter_context(tc.tile_pool(name="unread_pool", bufs=4))
-        xt_psum = ctx.enter_context(tc.psum_pool(name="xt_psum", bufs=2))
+        xt_psum = ctx.enter_context(tc.psum_pool(name="xt_psum", bufs=3))
         acc_psum = ctx.enter_context(tc.psum_pool(name="acc_psum", bufs=4))
+        scalar_psum = ctx.enter_context(tc.psum_pool(name="scalar_psum", bufs=1))
         ctx.enter_context(tc.manual_schedule())
 
         x_sb = [
@@ -91,16 +98,19 @@ def tile_modalityadaptivemodule_pa_kernel(
         one = keep.tile([P, 1], F32)
         unread_root = keep.tile([P, 1], F32)
         select = keep.tile([P, SELECT_COLUMNS], BF16)
-        stats = keep.tile([P, VECTOR_STATS_UNITS, UNIT_J, BN_STATS_DIM], F32)
-        mean_var = keep.tile([P, VECTOR_STATS_UNITS, UNIT_J, BN_AGGR_DIM], F32)
+        stats = keep.tile([P, N_UNITS, UNIT_J, BN_STATS_DIM], F32)
+        mean_var = keep.tile([P, N_UNITS, UNIT_J, BN_AGGR_DIM], F32)
         neg_mean = keep.tile([P, N_UNITS, UNIT_J], F32)
         sum_squares = keep.tile([P, N_UNITS, UNIT_J], F32)
         rstd = keep.tile([P, N_UNITS, UNIT_J], F32)
 
         xhat_of = {}
         xt_of = {}
+        planes_of = {}
         grouped_of = {}
         operand_of = {}
+        result_of = {}
+        scalar_acc_of = {}
 
         def block_view(dram, b):
             return dram[b].rearrange("(p j) c -> p j c", j=ROWS_PER_PARTITION)
@@ -113,8 +123,8 @@ def tile_modalityadaptivemodule_pa_kernel(
             source = block_view(streams[b // BLOCKS_PER_STREAM], b % BLOCKS_PER_STREAM)
             nc.sync.dma_start(out=x_sb[b][:, j0:j1, :], in_=source[:, j0:j1, :])
 
-        def load_biases():
-            for w in range(N_WEIGHTS):
+        def load_biases(s):
+            for w in WEIGHTS_FIRST_USED_BY[s]:
                 nc.sync.dma_start(
                     out=bias_rows[w : w + 1, :], in_=biases[w].rearrange("(o n) -> o n", o=1)
                 )
@@ -148,28 +158,34 @@ def tile_modalityadaptivemodule_pa_kernel(
 
         nc.scalar.activation(out=unread_root[:], in_=one[:], func=ACT.Sqrt)
 
+        def load_weight(w):
+            load_scales(w)
+            load_words(w)
+
         load_rows(0, 0, UNIT_J)
         load_rows(0, UNIT_J, ROWS_PER_PARTITION)
-        load_biases()
         load_vectors(0)
         load_rows(1, 0, ROWS_PER_PARTITION)
+        load_biases(0)
+        load_weight(0)
         load_rows(2, 0, ROWS_PER_PARTITION)
-        for w in WEIGHTS_FIRST_USED_BY[0]:
-            load_scales(w)
-        for w in WEIGHTS_FIRST_USED_BY[0]:
-            load_words(w)
+        load_weight(1)
+        load_weight(2)
         load_rows(3, 0, ROWS_PER_PARTITION)
-        load_vectors(1)
 
-        def prepare_stream(s):
+        def prepare_gain_shift(s):
             nc.scalar.copy(out=gain_shift[:, s, :, :], in_=gain_shift_bf[:, s, :, 0:PACK])
-            for w in WEIGHTS_FIRST_USED_BY[s]:
-                acc = acc_psum.tile([P, N_OUT], F32)
-                nc.tensor.matmul(
-                    out=acc[:], lhsT=select[:, w : w + 1].to_broadcast([P, P]), rhs=bias_rows[:],
-                    start=True, stop=True,
-                )
-                nc.scalar.copy(out=bias_all[:, w, :], in_=acc[:])
+
+        def spread_bias(w, pool):
+            acc = pool.tile([P, N_OUT], F32)
+            nc.tensor.matmul(
+                out=acc[:], lhsT=select[:, w : w + 1].to_broadcast([P, P]), rhs=bias_rows[:],
+                start=True, stop=True,
+            )
+            return acc
+
+        def keep_bias(w, acc):
+            nc.scalar.copy(out=bias_all[:, w, :], in_=acc[:])
 
         def statistics(u):
             b, j0 = unit_place(u)
@@ -178,13 +194,16 @@ def tile_modalityadaptivemodule_pa_kernel(
             for jj in range(UNIT_J):
                 nc.vector.bn_aggr(out=mean_var[:, u, jj, :], in_=stats[:, u, jj, :])
 
-        def statistics_on_scalar(u, jj):
+        def mean_on_scalar(u, jj):
             b, j0 = unit_place(u)
             scaled = unread_pool.tile([P, K], BF16)
             nc.scalar.activation(
                 out=scaled[:], in_=x_sb[b][:, j0 + jj, :], func=ACT.Identity,
                 scale=-1.0 / K, accum_out=neg_mean[:, u, jj : jj + 1],
             )
+
+        def squares_on_scalar(u, jj):
+            b, j0 = unit_place(u)
             squares = unread_pool.tile([P, K], BF16)
             nc.scalar.activation(
                 out=squares[:], in_=x_sb[b][:, j0 + jj, :], func=ACT.Square,
@@ -192,7 +211,7 @@ def tile_modalityadaptivemodule_pa_kernel(
             )
 
         def deviation(u):
-            if u < VECTOR_STATS_UNITS:
+            if u not in SCALAR_STATS:
                 nc.scalar.activation(
                     out=std[:, u, :], in_=mean_var[:, u, :, 1], func=ACT.Sqrt, bias=EPS
                 )
@@ -220,9 +239,10 @@ def tile_modalityadaptivemodule_pa_kernel(
 
         def transpose(u):
             xhat = xhat_of[u]
-            xt_lo = xt_psum.tile([P, 2, UNIT_ROWS], F32)
-            xt_hi = xt_psum.tile([P, 2, UNIT_ROWS], F32)
-            xt_of[u] = [xt_lo[:, 0, :], xt_lo[:, 1, :], xt_hi[:, 0, :], xt_hi[:, 1, :]]
+            xt_of[u] = []
+            for half in range(2):
+                xt = xt_psum.tile([P, 2, UNIT_ROWS], F32)
+                xt_of[u] += [xt[:, 0, :], xt[:, 1, :]]
             for jj in range(UNIT_J):
                 for t in range(PACK):
                     nc.tensor.transpose(
@@ -231,45 +251,41 @@ def tile_modalityadaptivemodule_pa_kernel(
                         identity=ident[:],
                     )
 
-        def scale_shift_by_row(u):
-            s = u // UNITS_PER_STREAM
+        def new_tn(u):
             planes = tn_pool.tile([P, PACK, UNIT_ROWS], BF16)
+            planes_of[u] = planes
             grouped = tn_pool.tile([P, UNIT_ROWS, PACK], BF16, align_bytes=64)
-            xt_rows = []
-            for jj in range(UNIT_J):
-                xt_lo = xt_psum.tile([P, PACK, P], F32)
-                xt_rows.append(xt_lo)
-                for t in range(PACK):
-                    nc.tensor.transpose(
-                        out=xt_lo[:, t, :], in_=xhat_of[u][:, jj, t, :], identity=ident[:]
-                    )
-            for jj in range(UNIT_J):
-                columns = slice(jj * P, (jj + 1) * P)
-                for t in range(PACK):
-                    nc.scalar.activation(
-                        out=planes[:, t, columns], in_=xt_rows[jj][:, t, :], func=ACT.Identity,
-                        scale=gain_shift[:, s, 0, t : t + 1], bias=gain_shift[:, s, 1, t : t + 1],
-                    )
-            nc.scalar.copy(
-                out=grouped[:].rearrange("p (c i) t -> p c t i", i=4),
-                in_=planes[:].rearrange("p t (c i) -> p c t i", i=4),
-            )
             grouped_of[u] = grouped
 
-        def scale_shift(u):
-            s = u // UNITS_PER_STREAM
-            planes = tn_pool.tile([P, PACK, UNIT_ROWS], BF16)
+        def transpose_row(u, jj):
+            xt = xt_psum.tile([P, PACK, P], F32)
             for t in range(PACK):
-                nc.scalar.activation(
-                    out=planes[:, t, :], in_=xt_of[u][t], func=ACT.Identity,
-                    scale=gain_shift[:, s, 0, t : t + 1], bias=gain_shift[:, s, 1, t : t + 1],
+                nc.tensor.transpose(
+                    out=xt[:, t, :], in_=xhat_of[u][:, jj, t, :], identity=ident[:]
                 )
-            grouped = tn_pool.tile([P, UNIT_ROWS, PACK], BF16, align_bytes=64)
-            nc.scalar.copy(
-                out=grouped[:].rearrange("p (c i) t -> p c t i", i=4),
-                in_=planes[:].rearrange("p t (c i) -> p c t i", i=4),
+            return xt
+
+        def scale_shift_plane(u, t, source, columns):
+            s = u // UNITS_PER_STREAM
+            nc.scalar.activation(
+                out=planes_of[u][:, t, columns], in_=source, func=ACT.Identity,
+                scale=gain_shift[:, s, 0, t : t + 1], bias=gain_shift[:, s, 1, t : t + 1],
             )
-            grouped_of[u] = grouped
+
+        def scale_shift_row(u, jj, xt):
+            for t in range(PACK):
+                scale_shift_plane(u, t, xt[:, t, :], slice(jj * P, (jj + 1) * P))
+
+        def group(u, copy=nc.scalar.copy):
+            copy(
+                out=grouped_of[u][:].rearrange("p (c i) t -> p c t i", i=4),
+                in_=planes_of[u][:].rearrange("p t (c i) -> p c t i", i=4),
+            )
+
+        def scale_shift(u):
+            new_tn(u)
+            for t in range(PACK):
+                scale_shift_plane(u, t, xt_of[u][t], slice(0, UNIT_ROWS))
 
         def quantise(u):
             codes = operand_pool.tile([P, UNIT_ROWS], U32, align_bytes=64)
@@ -281,73 +297,124 @@ def tile_modalityadaptivemodule_pa_kernel(
             )
             operand_of[u] = (codes, code_scales)
 
-        def project(u, o):
-            b, j0 = unit_place(u)
-            w = WEIGHTS_USED_BY[u // UNITS_PER_STREAM][o]
+        def multiply(u, o, jj, acc):
             codes, code_scales = operand_of[u]
-            result = result_pool.tile([P, UNIT_J, N_OUT], F32)
-            for jj in range(UNIT_J):
-                rows = slice(jj * P, (jj + 1) * P)
-                acc = acc_psum.tile([P, N_OUT], F32)
-                nc.tensor.matmul_mx(
-                    out=acc[:],
-                    lhsT=codes[:, rows].bitcast(FP8X4),
-                    lhsT_scale=code_scales[:, rows],
-                    rhs=w_words[:, w, :].bitcast(FP8X4),
-                    rhs_scale=w_scales[:, w, :],
-                    start=True,
-                    stop=True,
-                )
-                nc.vector.tensor_tensor(
-                    out=result[:, jj, :], in0=acc[:], in1=bias_all[:, w, :], op=ALU.add
-                )
-            nc.sync.dma_start(
-                out=block_view(outs[o], b)[:, j0 : j0 + UNIT_J, :], in_=result[:]
+            w = WEIGHTS_USED_BY[u // UNITS_PER_STREAM][o]
+            rows = slice(jj * P, (jj + 1) * P)
+            nc.tensor.matmul_mx(
+                out=acc[:],
+                lhsT=codes[:, rows].bitcast(FP8X4),
+                lhsT_scale=code_scales[:, rows],
+                rhs=w_words[:, w, :].bitcast(FP8X4),
+                rhs_scale=w_scales[:, w, :],
+                start=True,
+                stop=True,
             )
 
+        def bias_of(u, o):
+            return bias_all[:, WEIGHTS_USED_BY[u // UNITS_PER_STREAM][o], :]
+
+        def new_results(u):
+            for o in range(N_OUTPUTS):
+                result = result_pool.tile([P, UNIT_J, N_OUT], F32)
+                result_of[u, o] = result
+
+        def scalar_sum_pass(u, o, jj):
+            acc = scalar_psum.tile([P, N_OUT], F32)
+            multiply(u, o, jj, acc)
+            scalar_acc_of[u, o, jj] = acc
+
+        def scalar_sum(u, o, jj):
+            place = result_of[u, o][:, jj, :]
+            nc.scalar.copy(out=place, in_=scalar_acc_of[u, o, jj][:])
+            nc.gpsimd.tensor_tensor(out=place, in0=place, in1=bias_of(u, o), op=ALU.add)
+
+        def project(u, o):
+            for jj in range(UNIT_J):
+                if (o, jj) not in SCALAR_SUMS[u]:
+                    acc = acc_psum.tile([P, N_OUT], F32)
+                    multiply(u, o, jj, acc)
+                    nc.vector.tensor_tensor(
+                        out=result_of[u, o][:, jj, :], in0=acc[:], in1=bias_of(u, o), op=ALU.add
+                    )
+
+        def store(u, o):
+            b, j0 = unit_place(u)
+            nc.sync.dma_start(
+                out=block_view(outs[o], b)[:, j0 : j0 + UNIT_J, :], in_=result_of[u, o][:]
+            )
+
+        bias_accs = [spread_bias(w, acc_psum) for w in WEIGHTS_FIRST_USED_BY[0]]
+        mean_on_scalar(1, 0)
         statistics(0)
         deviation(0)
+        squares_on_scalar(1, 0)
         invert(0)
         normalise(0, nc.vector)
-        statistics(1)
-        prepare_stream(0)
+        prepare_gain_shift(0)
+        mean_on_scalar(1, 1)
+        squares_on_scalar(1, 1)
         deviation(1)
-        scale_shift_by_row(0)
+        xt_rows = [transpose_row(0, jj) for jj in range(UNIT_J)]
+        new_tn(0)
+        for jj in range(UNIT_J):
+            scale_shift_row(0, jj, xt_rows[jj])
         statistics(2)
         invert(1)
-        normalise(1)
-        statistics(3)
-        deviation(2)
+        normalise(1, nc.vector)
+        group(0, nc.vector.tensor_copy)
         quantise(0)
+        keep_bias(0, bias_accs[0])
+        deviation(2)
+        transpose(1)
+        scale_shift(1)
+        for w in WEIGHTS_FIRST_USED_BY[0][1:]:
+            keep_bias(w, bias_accs[w])
+        group(1)
+        statistics(3)
         invert(2)
         normalise(2)
         for u in range(N_UNITS):
+            new_results(u)
+            for place in SCALAR_SUMS[u]:
+                scalar_sum_pass(u, *place)
             if u == 0:
                 project(0, 0)
-                transpose(1)
-            if u + 1 < N_UNITS:
+                store(0, 0)
+            if 0 < u < N_UNITS - 1:
                 scale_shift(u + 1)
+            for place in SCALAR_SUMS[u]:
+                scalar_sum(u, *place)
+            if 0 < u < N_UNITS - 1:
+                group(u + 1)
             if u + 3 < N_UNITS:
                 deviation(u + 3)
-            if u < SCALAR_STATS_UNITS * UNIT_J:
-                statistics_on_scalar(VECTOR_STATS_UNITS + u // UNIT_J, u % UNIT_J)
+            for row in SCALAR_ROWS[u]:
+                mean_on_scalar(*row)
+                squares_on_scalar(*row)
             if u > 0:
                 project(u, 0)
-            if FIRST_STATS_UNITS + u < VECTOR_STATS_UNITS:
-                statistics(FIRST_STATS_UNITS + u)
+                store(u, 0)
+            for v in VECTOR_UNITS[u]:
+                statistics(v)
             project(u, 1)
+            store(u, 1)
             if u == 0:
-                for w in WEIGHTS_FIRST_USED_BY[1]:
-                    load_scales(w)
-                for w in WEIGHTS_FIRST_USED_BY[1]:
-                    load_words(w)
+                load_weight(3)
             if u + 1 < N_UNITS:
                 quantise(u + 1)
             if u + 3 < N_UNITS:
                 invert(u + 3)
                 normalise(u + 3)
             project(u, 2)
+            store(u, 2)
+            if u == 0:
+                load_weight(4)
+                load_vectors(1)
+                load_biases(1)
             if u + 2 < N_UNITS:
-                if (u + 2) % UNITS_PER_STREAM == 0:
-                    prepare_stream((u + 2) // UNITS_PER_STREAM)
+                if u + 2 == UNITS_PER_STREAM:
+                    prepare_gain_shift(1)
+                    for w in WEIGHTS_FIRST_USED_BY[1]:
+                        keep_bias(w, spread_bias(w, scalar_psum))
                 transpose(u + 2)

@@ -41,10 +41,11 @@ BN_STATS_DIM = 6
 BN_AGGR_DIM = 2
 VECTOR_PAD = 16
 
-SCALAR_STATS = (1, 6, 7)
+SCALAR_STATS = (1, 5, 6, 7)
 
-SCALAR_ROWS = (((6, 0),), ((6, 1),), ((7, 0),), ((7, 1),), (), (), (), ())
-VECTOR_UNITS = ((4,), (5,), (), (), (), (), (), ())
+GROUPED_ON_GPSIMD = (2, 3, 4)
+SCALAR_ROWS = (((5, 0),), ((5, 1), (6, 0)), ((6, 1),), ((7, 0), (7, 1)), (), (), (), ())
+VECTOR_UNITS = ((4,), (), (), (), (), (), (), ())
 NO_SUMS = ()
 ONE_SUM = ((1, 1),)
 TWO_SUMS = ((1, 1), (2, 1))
@@ -276,6 +277,12 @@ def tile_modalityadaptivemodule_pa_kernel(
             for t in range(PACK):
                 scale_shift_plane(u, t, xt[:, t, :], slice(jj * P, (jj + 1) * P))
 
+        def group_on_gpsimd(u):
+            nc.gpsimd.tensor_scalar(
+                out=grouped_of[u][:], in0=planes_of[u][:].rearrange("p t c -> p c t"),
+                scalar1=1.0, scalar2=0.0, op0=ALU.mult, op1=ALU.add,
+            )
+
         def group(u, copy=nc.scalar.copy):
             copy(
                 out=grouped_of[u][:].rearrange("p (c i) t -> p c t i", i=4),
@@ -386,7 +393,10 @@ def tile_modalityadaptivemodule_pa_kernel(
             for place in SCALAR_SUMS[u]:
                 scalar_sum(u, *place)
             if 0 < u < N_UNITS - 1:
-                group(u + 1)
+                if u + 1 in GROUPED_ON_GPSIMD:
+                    group_on_gpsimd(u + 1)
+                else:
+                    group(u + 1)
             if u + 3 < N_UNITS:
                 deviation(u + 3)
             for row in SCALAR_ROWS[u]:

@@ -46,6 +46,7 @@ SCALAR_STATS = (1, 5, 6, 7)
 GROUPED_ON_GPSIMD = (2, 3, 4)
 SCALAR_ROWS = (((5, 0),), ((5, 1), (6, 0)), ((6, 1),), ((7, 0), (7, 1)), (), (), (), ())
 VECTOR_UNITS = ((4,), (), (), (), (), (), (), ())
+LOADS_PER_STORE = 2
 NO_SUMS = ()
 ONE_SUM = ((1, 1),)
 TWO_SUMS = ((1, 1), (2, 1))
@@ -124,32 +125,37 @@ def tile_modalityadaptivemodule_pa_kernel(
             source = block_view(streams[b // BLOCKS_PER_STREAM], b % BLOCKS_PER_STREAM)
             nc.sync.dma_start(out=x_sb[b][:, j0:j1, :], in_=source[:, j0:j1, :])
 
-        def load_biases(s):
-            for w in WEIGHTS_FIRST_USED_BY[s]:
-                nc.sync.dma_start(
-                    out=bias_rows[w : w + 1, :], in_=biases[w].rearrange("(o n) -> o n", o=1)
-                )
+        def load_bias(w):
+            nc.sync.dma_start(
+                out=bias_rows[w : w + 1, :], in_=biases[w].rearrange("(o n) -> o n", o=1)
+            )
 
-        def load_vectors(s):
+        def load_vector(s, i):
             with nc.allow_non_contiguous_dma(reason="four bfloat16 values to a partition"):
-                for i in range(2):
-                    nc.sync.dma_start(
-                        out=gain_shift_bf[:, s, i, 0:PACK],
-                        in_=gains_shifts[s][i].rearrange("(p t) -> p t", t=PACK),
-                    )
-
-        def load_scales(w):
-            for quad in range(SCALE_ROWS // PACK):
                 nc.sync.dma_start(
-                    out=w_scales[QUADRANT * quad : QUADRANT * quad + PACK, w, :].bitcast(I32),
-                    in_=weight_scales[w][0, PACK * quad : PACK * (quad + 1), :].bitcast(I32),
+                    out=gain_shift_bf[:, s, i, 0:PACK],
+                    in_=gains_shifts[s][i].rearrange("(p t) -> p t", t=PACK),
                 )
+
+        def load_scales(w, quad):
+            nc.sync.dma_start(
+                out=w_scales[QUADRANT * quad : QUADRANT * quad + PACK, w, :].bitcast(I32),
+                in_=weight_scales[w][0, PACK * quad : PACK * (quad + 1), :].bitcast(I32),
+            )
 
         def load_words(w):
             nc.sync.dma_start(
                 out=w_words[:, w, :].bitcast(I32),
                 in_=weight_words[w][0].rearrange("p n t -> p (n t)").bitcast(I32),
             )
+
+        def weight_loads(w):
+            quads = SCALE_ROWS // PACK
+            return [(load_scales, w, quad) for quad in range(quads)] + [(load_words, w)]
+
+        def issue(loads):
+            for load, *what in loads:
+                load(*what)
 
         nc.gpsimd.memset(one[:], 1.0)
         nc.gpsimd.memset(bias_rows[:].bitcast(I32), 0)
@@ -159,20 +165,21 @@ def tile_modalityadaptivemodule_pa_kernel(
 
         nc.scalar.activation(out=unread_root[:], in_=one[:], func=ACT.Sqrt)
 
-        def load_weight(w):
-            load_scales(w)
-            load_words(w)
-
         load_rows(0, 0, UNIT_J)
         load_rows(0, UNIT_J, ROWS_PER_PARTITION)
-        load_vectors(0)
+        issue([(load_vector, 0, i) for i in range(2)])
         load_rows(1, 0, ROWS_PER_PARTITION)
-        load_biases(0)
-        load_weight(0)
+        issue([(load_bias, w) for w in WEIGHTS_FIRST_USED_BY[0]])
+        issue(weight_loads(0))
         load_rows(2, 0, ROWS_PER_PARTITION)
-        load_weight(1)
-        load_weight(2)
+        issue(weight_loads(1))
+        issue(weight_loads(2))
         load_rows(3, 0, ROWS_PER_PARTITION)
+        later_loads = [(load_vector, 1, i) for i in range(2)]
+        for w in WEIGHTS_FIRST_USED_BY[1]:
+            later_loads.append((load_bias, w))
+        for w in WEIGHTS_FIRST_USED_BY[1]:
+            later_loads += weight_loads(w)
 
         def prepare_gain_shift(s):
             nc.scalar.copy(out=gain_shift[:, s, :, :], in_=gain_shift_bf[:, s, :, 0:PACK])
@@ -226,11 +233,11 @@ def tile_modalityadaptivemodule_pa_kernel(
         def invert(u):
             nc.vector.reciprocal(out=rstd[:, u, :], in_=std[:, u, :])
 
-        def normalise(u, engine=nc.gpsimd):
+        def normalise(u, engines=(nc.gpsimd, nc.gpsimd)):
             b, j0 = unit_place(u)
             xhat = xhat_pool.tile([P, UNIT_J, PACK, P], F32)
             for jj in range(UNIT_J):
-                engine.tensor_scalar(
+                engines[jj].tensor_scalar(
                     out=xhat[:, jj, :, :],
                     in0=x_sb[b][:, j0 + jj, :].rearrange("p (q t) -> p t q", t=PACK),
                     scalar1=neg_mean[:, u, jj : jj + 1], scalar2=rstd[:, u, jj : jj + 1],
@@ -350,6 +357,8 @@ def tile_modalityadaptivemodule_pa_kernel(
             nc.sync.dma_start(
                 out=block_view(outs[o], b)[:, j0 : j0 + UNIT_J, :], in_=result_of[u, o][:]
             )
+            issue(later_loads[:LOADS_PER_STORE])
+            later_loads[:] = later_loads[LOADS_PER_STORE:]
 
         bias_accs = [spread_bias(w, acc_psum) for w in WEIGHTS_FIRST_USED_BY[0]]
         mean_on_scalar(1, 0)
@@ -357,7 +366,7 @@ def tile_modalityadaptivemodule_pa_kernel(
         deviation(0)
         squares_on_scalar(1, 0)
         invert(0)
-        normalise(0, nc.vector)
+        normalise(0, (nc.vector, nc.vector))
         prepare_gain_shift(0)
         mean_on_scalar(1, 1)
         squares_on_scalar(1, 1)
@@ -368,7 +377,7 @@ def tile_modalityadaptivemodule_pa_kernel(
             scale_shift_row(0, jj, xt_rows[jj])
         statistics(2)
         invert(1)
-        normalise(1, nc.vector)
+        normalise(1, (nc.vector, nc.vector))
         group(0, nc.vector.tensor_copy)
         quantise(0)
         keep_bias(0, bias_accs[0])
@@ -409,8 +418,6 @@ def tile_modalityadaptivemodule_pa_kernel(
                 statistics(v)
             project(u, 1)
             store(u, 1)
-            if u == 0:
-                load_weight(3)
             if u + 1 < N_UNITS:
                 quantise(u + 1)
             if u + 3 < N_UNITS:
@@ -418,13 +425,10 @@ def tile_modalityadaptivemodule_pa_kernel(
                 normalise(u + 3)
             project(u, 2)
             store(u, 2)
-            if u == 0:
-                load_weight(4)
-                load_vectors(1)
-                load_biases(1)
             if u + 2 < N_UNITS:
+                if u in (1, 2):
+                    w = WEIGHTS_FIRST_USED_BY[1][u - 1]
+                    keep_bias(w, spread_bias(w, scalar_psum))
                 if u + 2 == UNITS_PER_STREAM:
                     prepare_gain_shift(1)
-                    for w in WEIGHTS_FIRST_USED_BY[1]:
-                        keep_bias(w, spread_bias(w, scalar_psum))
                 transpose(u + 2)

@@ -45,12 +45,11 @@ SCALAR_STATS = (1, 5, 6, 7)
 
 GROUPED_ON_GPSIMD = (2, 3, 4)
 SCALAR_ROWS = (((5, 0),), ((5, 1), (6, 0)), ((6, 1),), ((7, 0), (7, 1)), (), (), (), ())
-VECTOR_UNITS = ((4,), (), (), (), (), (), (), ())
 LOADS_PER_STORE = 2
 NO_SUMS = ()
 ONE_SUM = ((1, 1),)
 TWO_SUMS = ((1, 1), (2, 1))
-SCALAR_SUMS = (NO_SUMS, NO_SUMS, NO_SUMS, NO_SUMS, NO_SUMS, ONE_SUM, ONE_SUM, ONE_SUM)
+SCALAR_SUMS = (NO_SUMS, NO_SUMS, NO_SUMS, NO_SUMS, ONE_SUM, ONE_SUM, ONE_SUM, NO_SUMS)
 
 FLOPS = 2 * N_BLOCKS * BLOCK_ROWS * K * 3 * N_OUT
 
@@ -94,7 +93,7 @@ def tile_modalityadaptivemodule_pa_kernel(
         gain_shift_bf = keep.tile([P, 2, 2, VECTOR_PAD], BF16)
         gain_shift = keep.tile([P, 2, 2, PACK], F32)
         bias_rows = keep.tile([P, N_OUT], BF16)
-        bias_all = keep.tile([P, N_WEIGHTS, N_OUT], F32)
+        bias_all = keep.tile([P, N_WEIGHTS, N_OUT], BF16)
         ident = keep.tile([P, P], F32)
         std = keep.tile([P, N_UNITS, UNIT_J], F32)
         one = keep.tile([P, 1], F32)
@@ -165,7 +164,8 @@ def tile_modalityadaptivemodule_pa_kernel(
 
         nc.scalar.activation(out=unread_root[:], in_=one[:], func=ACT.Sqrt)
 
-        load_rows(0, 0, UNIT_J)
+        load_rows(0, 0, 1)
+        load_rows(0, 1, UNIT_J)
         load_rows(0, UNIT_J, ROWS_PER_PARTITION)
         issue([(load_vector, 0, i) for i in range(2)])
         load_rows(1, 0, ROWS_PER_PARTITION)
@@ -185,7 +185,7 @@ def tile_modalityadaptivemodule_pa_kernel(
             nc.scalar.copy(out=gain_shift[:, s, :, :], in_=gain_shift_bf[:, s, :, 0:PACK])
 
         def spread_bias(w, pool):
-            acc = pool.tile([P, N_OUT], F32)
+            acc = pool.tile([P, N_OUT], BF16)
             nc.tensor.matmul(
                 out=acc[:], lhsT=select[:, w : w + 1].to_broadcast([P, P]), rhs=bias_rows[:],
                 start=True, stop=True,
@@ -195,12 +195,18 @@ def tile_modalityadaptivemodule_pa_kernel(
         def keep_bias(w, acc):
             nc.scalar.copy(out=bias_all[:, w, :], in_=acc[:])
 
-        def statistics(u):
+        def row_statistics(u, jj):
             b, j0 = unit_place(u)
-            for jj in range(UNIT_J):
-                nc.vector.bn_stats(out=stats[:, u, jj, :], in_=x_sb[b][:, j0 + jj, :])
+            nc.vector.bn_stats(out=stats[:, u, jj, :], in_=x_sb[b][:, j0 + jj, :])
+
+        def aggregate(u):
             for jj in range(UNIT_J):
                 nc.vector.bn_aggr(out=mean_var[:, u, jj, :], in_=stats[:, u, jj, :])
+
+        def statistics(u):
+            for jj in range(UNIT_J):
+                row_statistics(u, jj)
+            aggregate(u)
 
         def mean_on_scalar(u, jj):
             b, j0 = unit_place(u)
@@ -360,7 +366,6 @@ def tile_modalityadaptivemodule_pa_kernel(
             issue(later_loads[:LOADS_PER_STORE])
             later_loads[:] = later_loads[LOADS_PER_STORE:]
 
-        bias_accs = [spread_bias(w, acc_psum) for w in WEIGHTS_FIRST_USED_BY[0]]
         mean_on_scalar(1, 0)
         statistics(0)
         deviation(0)
@@ -372,12 +377,14 @@ def tile_modalityadaptivemodule_pa_kernel(
         squares_on_scalar(1, 1)
         deviation(1)
         xt_rows = [transpose_row(0, jj) for jj in range(UNIT_J)]
+        bias_accs = [spread_bias(w, acc_psum) for w in WEIGHTS_FIRST_USED_BY[0]]
         new_tn(0)
         for jj in range(UNIT_J):
             scale_shift_row(0, jj, xt_rows[jj])
         statistics(2)
         invert(1)
-        normalise(1, (nc.vector, nc.vector))
+        normalise(1)
+        statistics(3)
         group(0, nc.vector.tensor_copy)
         quantise(0)
         keep_bias(0, bias_accs[0])
@@ -387,9 +394,9 @@ def tile_modalityadaptivemodule_pa_kernel(
         for w in WEIGHTS_FIRST_USED_BY[0][1:]:
             keep_bias(w, bias_accs[w])
         group(1)
-        statistics(3)
         invert(2)
         normalise(2)
+        row_statistics(4, 0)
         for u in range(N_UNITS):
             new_results(u)
             for place in SCALAR_SUMS[u]:
@@ -414,8 +421,9 @@ def tile_modalityadaptivemodule_pa_kernel(
             if u > 0:
                 project(u, 0)
                 store(u, 0)
-            for v in VECTOR_UNITS[u]:
-                statistics(v)
+            if u == 0:
+                row_statistics(4, 1)
+                aggregate(4)
             project(u, 1)
             store(u, 1)
             if u + 1 < N_UNITS:

@@ -93,7 +93,7 @@ def tile_modalityadaptivemodule_pa_kernel(
         gain_shift_bf = keep.tile([P, 2, 2, VECTOR_PAD], BF16)
         gain_shift = keep.tile([P, 2, 2, PACK], F32)
         bias_rows = keep.tile([P, N_OUT], BF16)
-        bias_all = keep.tile([P, N_WEIGHTS, N_OUT], BF16)
+        bias_all = keep.tile([P, N_WEIGHTS, N_OUT], F32)
         ident = keep.tile([P, P], F32)
         std = keep.tile([P, N_UNITS, UNIT_J], F32)
         one = keep.tile([P, 1], F32)
@@ -173,19 +173,22 @@ def tile_modalityadaptivemodule_pa_kernel(
         issue(weight_loads(0))
         load_rows(2, 0, ROWS_PER_PARTITION)
         issue(weight_loads(1))
-        issue(weight_loads(2))
+        load_words(2)
+        load_words(3)
+        issue(weight_loads(2)[:4])
         load_rows(3, 0, ROWS_PER_PARTITION)
+        load_words(4)
         later_loads = [(load_vector, 1, i) for i in range(2)]
         for w in WEIGHTS_FIRST_USED_BY[1]:
             later_loads.append((load_bias, w))
         for w in WEIGHTS_FIRST_USED_BY[1]:
-            later_loads += weight_loads(w)
+            later_loads += weight_loads(w)[:4]
 
         def prepare_gain_shift(s):
             nc.scalar.copy(out=gain_shift[:, s, :, :], in_=gain_shift_bf[:, s, :, 0:PACK])
 
         def spread_bias(w, pool):
-            acc = pool.tile([P, N_OUT], BF16)
+            acc = pool.tile([P, N_OUT], F32)
             nc.tensor.matmul(
                 out=acc[:], lhsT=select[:, w : w + 1].to_broadcast([P, P]), rhs=bias_rows[:],
                 start=True, stop=True,

@@ -41,9 +41,7 @@ BN_STATS_DIM = 6
 BN_AGGR_DIM = 2
 VECTOR_PAD = 16
 
-SCALAR_STATS = (1, 5, 6, 7)
-
-GROUPED_ON_GPSIMD = (2, 3, 4)
+GROUPED_ON_GPSIMD = (1, 2, 3, 4)
 SCALAR_ROWS = (((5, 0),), ((5, 1), (6, 0)), ((6, 1),), ((7, 0), (7, 1)), (), (), (), ())
 LOADS_PER_STORE = 2
 NO_SUMS = ()
@@ -105,6 +103,7 @@ def tile_modalityadaptivemodule_pa_kernel(
         sum_squares = keep.tile([P, N_UNITS, UNIT_J], F32)
         rstd = keep.tile([P, N_UNITS, UNIT_J], F32)
 
+        by_vector = set()
         xhat_of = {}
         xt_of = {}
         planes_of = {}
@@ -165,24 +164,23 @@ def tile_modalityadaptivemodule_pa_kernel(
         nc.scalar.activation(out=unread_root[:], in_=one[:], func=ACT.Sqrt)
 
         load_rows(0, 0, 1)
+        load_bias(0)
+        load_bias(1)
         load_rows(0, 1, UNIT_J)
+        load_bias(2)
         load_rows(0, UNIT_J, ROWS_PER_PARTITION)
-        issue([(load_vector, 0, i) for i in range(2)])
         load_rows(1, 0, ROWS_PER_PARTITION)
-        issue([(load_bias, w) for w in WEIGHTS_FIRST_USED_BY[0]])
-        issue(weight_loads(0))
+        issue([(load_vector, 0, i) for i in range(2)])
         load_rows(2, 0, ROWS_PER_PARTITION)
+        issue(weight_loads(0))
         issue(weight_loads(1))
-        load_words(2)
-        load_words(3)
-        issue(weight_loads(2)[:4])
+        issue(weight_loads(2))
         load_rows(3, 0, ROWS_PER_PARTITION)
-        load_words(4)
         later_loads = [(load_vector, 1, i) for i in range(2)]
         for w in WEIGHTS_FIRST_USED_BY[1]:
             later_loads.append((load_bias, w))
         for w in WEIGHTS_FIRST_USED_BY[1]:
-            later_loads += weight_loads(w)[:4]
+            later_loads += weight_loads(w)
 
         def prepare_gain_shift(s):
             nc.scalar.copy(out=gain_shift[:, s, :, :], in_=gain_shift_bf[:, s, :, 0:PACK])
@@ -202,9 +200,13 @@ def tile_modalityadaptivemodule_pa_kernel(
             b, j0 = unit_place(u)
             nc.vector.bn_stats(out=stats[:, u, jj, :], in_=x_sb[b][:, j0 + jj, :])
 
+        def aggregate_row(u, jj):
+            nc.vector.bn_aggr(out=mean_var[:, u, jj, :], in_=stats[:, u, jj, :])
+            by_vector.add((u, jj))
+
         def aggregate(u):
             for jj in range(UNIT_J):
-                nc.vector.bn_aggr(out=mean_var[:, u, jj, :], in_=stats[:, u, jj, :])
+                aggregate_row(u, jj)
 
         def statistics(u):
             for jj in range(UNIT_J):
@@ -227,17 +229,34 @@ def tile_modalityadaptivemodule_pa_kernel(
                 bias=neg_mean[:, u, jj : jj + 1], accum_out=sum_squares[:, u, jj : jj + 1],
             )
 
+        def statistics_on_scalar(u, jj):
+            mean_on_scalar(u, jj)
+            squares_on_scalar(u, jj)
+
         def deviation(u):
-            if u not in SCALAR_STATS:
+            kinds = [(u, jj) in by_vector for jj in range(UNIT_J)]
+            if all(kinds):
                 nc.scalar.activation(
                     out=std[:, u, :], in_=mean_var[:, u, :, 1], func=ACT.Sqrt, bias=EPS
                 )
                 nc.scalar.mul(out=neg_mean[:, u, :], in_=mean_var[:, u, :, 0], mul=-1.0)
-            else:
+            elif not any(kinds):
                 nc.scalar.activation(
                     out=std[:, u, :], in_=sum_squares[:, u, :], func=ACT.Sqrt,
                     scale=1.0 / K, bias=EPS,
                 )
+            else:
+                for jj in range(UNIT_J):
+                    if kinds[jj]:
+                        nc.scalar.activation(
+                            out=std[:, u, jj : jj + 1], in_=mean_var[:, u, jj, 1:2], func=ACT.Sqrt, bias=EPS
+                        )
+                        nc.scalar.mul(out=neg_mean[:, u, jj : jj + 1], in_=mean_var[:, u, jj, 0:1], mul=-1.0)
+                    else:
+                        nc.scalar.activation(
+                            out=std[:, u, jj : jj + 1], in_=sum_squares[:, u, jj : jj + 1], func=ACT.Sqrt,
+                            scale=1.0 / K, bias=EPS,
+                        )
 
         def invert(u):
             nc.vector.reciprocal(out=rstd[:, u, :], in_=std[:, u, :])
@@ -310,15 +329,32 @@ def tile_modalityadaptivemodule_pa_kernel(
             for t in range(PACK):
                 scale_shift_plane(u, t, xt_of[u][t], slice(0, UNIT_ROWS))
 
-        def quantise(u):
+        def new_operand(u):
             codes = operand_pool.tile([P, UNIT_ROWS], U32, align_bytes=64)
             code_scales = operand_pool.tile([P, UNIT_ROWS], U8, align_bytes=64)
-            nc.vector.quantize_mx(
-                out=codes[:].bitcast(FP8X4),
-                scales=code_scales[:],
-                in_=grouped_of[u][:].rearrange("p c t -> p (c t)"),
-            )
             operand_of[u] = (codes, code_scales)
+
+        def quantise_columns(u, columns):
+            codes, code_scales = operand_of[u]
+            nc.vector.quantize_mx(
+                out=codes[:, columns].bitcast(FP8X4),
+                scales=code_scales[:, columns],
+                in_=grouped_of[u][:, columns, :].rearrange("p c t -> p (c t)"),
+            )
+
+        def group_row(u, jj):
+            columns = slice(jj * P, (jj + 1) * P)
+            nc.vector.tensor_copy(
+                out=grouped_of[u][:, columns, :].rearrange("p (c i) t -> p c t i", i=4),
+                in_=planes_of[u][:, :, columns].rearrange("p t (c i) -> p c t i", i=4),
+            )
+
+        def quantise_row(u, jj):
+            quantise_columns(u, slice(jj * P, (jj + 1) * P))
+
+        def quantise(u):
+            new_operand(u)
+            quantise_columns(u, slice(0, UNIT_ROWS))
 
         def multiply(u, o, jj, acc):
             codes, code_scales = operand_of[u]
@@ -361,6 +397,21 @@ def tile_modalityadaptivemodule_pa_kernel(
                         out=result_of[u, o][:, jj, :], in0=acc[:], in1=bias_of(u, o), op=ALU.add
                     )
 
+        def project_one(u, o, jj):
+            acc = acc_psum.tile([P, N_OUT], F32)
+            multiply(u, o, jj, acc)
+            nc.vector.tensor_tensor(
+                out=result_of[u, o][:, jj, :], in0=acc[:], in1=bias_of(u, o), op=ALU.add
+            )
+
+        def store_row(u, o, jj):
+            b, j0 = unit_place(u)
+            nc.sync.dma_start(
+                out=block_view(outs[o], b)[:, j0 + jj, :], in_=result_of[u, o][:, jj, :]
+            )
+            issue(later_loads[:1])
+            later_loads[:] = later_loads[1:]
+
         def store(u, o):
             b, j0 = unit_place(u)
             nc.sync.dma_start(
@@ -369,44 +420,53 @@ def tile_modalityadaptivemodule_pa_kernel(
             issue(later_loads[:LOADS_PER_STORE])
             later_loads[:] = later_loads[LOADS_PER_STORE:]
 
-        mean_on_scalar(1, 0)
-        statistics(0)
+        row_statistics(0, 0)
+        row_statistics(0, 1)
+        row_statistics(1, 0)
+        aggregate(0)
+        bias_accs = [spread_bias(w, acc_psum) for w in (0, 1)]
+        keep_bias(0, bias_accs[0])
         deviation(0)
-        squares_on_scalar(1, 0)
-        invert(0)
-        normalise(0, (nc.vector, nc.vector))
+        keep_bias(1, bias_accs[1])
         prepare_gain_shift(0)
-        mean_on_scalar(1, 1)
-        squares_on_scalar(1, 1)
+        row_statistics(1, 1)
+        invert(0)
+        aggregate(1)
         deviation(1)
-        xt_rows = [transpose_row(0, jj) for jj in range(UNIT_J)]
-        bias_accs = [spread_bias(w, acc_psum) for w in WEIGHTS_FIRST_USED_BY[0]]
-        new_tn(0)
-        for jj in range(UNIT_J):
-            scale_shift_row(0, jj, xt_rows[jj])
-        statistics(2)
+        normalise(0, (nc.gpsimd, nc.vector))
+        row_statistics(3, 0)
         invert(1)
         normalise(1)
-        statistics(3)
-        group(0, nc.vector.tensor_copy)
-        quantise(0)
-        keep_bias(0, bias_accs[0])
+        statistics_on_scalar(2, 0)
+        row_statistics(2, 1)
+        row_statistics(3, 1)
+        aggregate_row(2, 1)
+        aggregate(3)
+        xt_rows = [transpose_row(0, jj) for jj in range(UNIT_J)]
+        new_tn(0)
+        new_operand(0)
         deviation(2)
+        scale_shift_row(0, 0, xt_rows[0])
+        row_statistics(4, 0)
+        invert(2)
+        group_row(0, 0)
+        normalise(2)
+        quantise_row(0, 0)
+        scale_shift_row(0, 1, xt_rows[1])
+        row_statistics(4, 1)
+        group_row(0, 1)
+        aggregate(4)
+        quantise_row(0, 1)
+        keep_bias(2, spread_bias(2, acc_psum))
         transpose(1)
         scale_shift(1)
-        for w in WEIGHTS_FIRST_USED_BY[0][1:]:
-            keep_bias(w, bias_accs[w])
-        group(1)
-        invert(2)
-        normalise(2)
-        row_statistics(4, 0)
+        group_on_gpsimd(1)
+        deviation(3)
+        deviation(4)
         for u in range(N_UNITS):
             new_results(u)
             for place in SCALAR_SUMS[u]:
                 scalar_sum_pass(u, *place)
-            if u == 0:
-                project(0, 0)
-                store(0, 0)
             if 0 < u < N_UNITS - 1:
                 scale_shift(u + 1)
             for place in SCALAR_SUMS[u]:
@@ -416,17 +476,26 @@ def tile_modalityadaptivemodule_pa_kernel(
                     group_on_gpsimd(u + 1)
                 else:
                     group(u + 1)
-            if u + 3 < N_UNITS:
+            if 4 < u + 3 < N_UNITS:
                 deviation(u + 3)
             for row in SCALAR_ROWS[u]:
-                mean_on_scalar(*row)
-                squares_on_scalar(*row)
-            if u > 0:
-                project(u, 0)
-                store(u, 0)
+                statistics_on_scalar(*row)
             if u == 0:
-                row_statistics(4, 1)
-                aggregate(4)
+                for o in range(N_OUTPUTS):
+                    project_one(0, o, 0)
+                    store_row(0, o, 0)
+                invert(3)
+                normalise(3)
+                project_one(0, 0, 1)
+                store_row(0, 0, 1)
+                quantise(1)
+                for o in (1, 2):
+                    project_one(0, o, 1)
+                    store_row(0, o, 1)
+                transpose(2)
+                continue
+            project(u, 0)
+            store(u, 0)
             project(u, 1)
             store(u, 1)
             if u + 1 < N_UNITS:

@@ -41,13 +41,13 @@ BN_STATS_DIM = 6
 BN_AGGR_DIM = 2
 VECTOR_PAD = 16
 
-GROUPED_ON_GPSIMD = (1, 2, 3, 4)
+GROUPED_ON_GPSIMD = (2, 3, 4)
 SCALAR_ROWS = (((5, 0),), ((5, 1), (6, 0)), ((6, 1),), ((7, 0), (7, 1)), (), (), (), ())
 LOADS_PER_STORE = 2
 NO_SUMS = ()
 ONE_SUM = ((1, 1),)
 TWO_SUMS = ((1, 1), (2, 1))
-SCALAR_SUMS = (NO_SUMS, NO_SUMS, NO_SUMS, NO_SUMS, ONE_SUM, ONE_SUM, ONE_SUM, NO_SUMS)
+SCALAR_SUMS = (NO_SUMS, NO_SUMS, NO_SUMS, NO_SUMS, NO_SUMS, ONE_SUM, ONE_SUM, NO_SUMS)
 
 FLOPS = 2 * N_BLOCKS * BLOCK_ROWS * K * 3 * N_OUT
 
@@ -164,13 +164,12 @@ def tile_modalityadaptivemodule_pa_kernel(
         nc.scalar.activation(out=unread_root[:], in_=one[:], func=ACT.Sqrt)
 
         load_rows(0, 0, 1)
-        load_bias(0)
-        load_bias(1)
         load_rows(0, 1, UNIT_J)
-        load_bias(2)
         load_rows(0, UNIT_J, ROWS_PER_PARTITION)
-        load_rows(1, 0, ROWS_PER_PARTITION)
+        load_rows(1, 0, UNIT_J)
+        load_rows(1, UNIT_J, ROWS_PER_PARTITION)
         issue([(load_vector, 0, i) for i in range(2)])
+        issue([(load_bias, w) for w in WEIGHTS_FIRST_USED_BY[0]])
         load_rows(2, 0, ROWS_PER_PARTITION)
         issue(weight_loads(0))
         issue(weight_loads(1))
@@ -420,49 +419,47 @@ def tile_modalityadaptivemodule_pa_kernel(
             issue(later_loads[:LOADS_PER_STORE])
             later_loads[:] = later_loads[LOADS_PER_STORE:]
 
+        mean_on_scalar(1, 0)
         row_statistics(0, 0)
         row_statistics(0, 1)
-        row_statistics(1, 0)
         aggregate(0)
-        bias_accs = [spread_bias(w, acc_psum) for w in (0, 1)]
-        keep_bias(0, bias_accs[0])
         deviation(0)
-        keep_bias(1, bias_accs[1])
-        prepare_gain_shift(0)
-        row_statistics(1, 1)
+        mean_on_scalar(1, 1)
+        row_statistics(2, 0)
         invert(0)
-        aggregate(1)
+        normalise(0, (nc.vector, nc.vector))
+        squares_on_scalar(1, 0)
+        squares_on_scalar(1, 1)
+        prepare_gain_shift(0)
         deviation(1)
-        normalise(0, (nc.gpsimd, nc.vector))
-        row_statistics(3, 0)
+        row_statistics(2, 1)
+        aggregate(2)
         invert(1)
         normalise(1)
-        statistics_on_scalar(2, 0)
-        row_statistics(2, 1)
-        row_statistics(3, 1)
-        aggregate_row(2, 1)
-        aggregate(3)
         xt_rows = [transpose_row(0, jj) for jj in range(UNIT_J)]
         new_tn(0)
         new_operand(0)
-        deviation(2)
         scale_shift_row(0, 0, xt_rows[0])
-        row_statistics(4, 0)
-        invert(2)
-        group_row(0, 0)
-        normalise(2)
-        quantise_row(0, 0)
+        deviation(2)
         scale_shift_row(0, 1, xt_rows[1])
+        row_statistics(3, 0)
+        row_statistics(3, 1)
+        row_statistics(4, 0)
+        aggregate(3)
+        for jj in range(UNIT_J):
+            group_row(0, jj)
+        for jj in range(UNIT_J):
+            quantise_row(0, jj)
+        invert(2)
+        normalise(2)
+        bias_accs = [spread_bias(w, acc_psum) for w in WEIGHTS_FIRST_USED_BY[0]]
+        for w in WEIGHTS_FIRST_USED_BY[0]:
+            keep_bias(w, bias_accs[w])
         row_statistics(4, 1)
-        group_row(0, 1)
-        aggregate(4)
-        quantise_row(0, 1)
-        keep_bias(2, spread_bias(2, acc_psum))
         transpose(1)
         scale_shift(1)
-        group_on_gpsimd(1)
+        group(1)
         deviation(3)
-        deviation(4)
         for u in range(N_UNITS):
             new_results(u)
             for place in SCALAR_SUMS[u]:
@@ -484,11 +481,13 @@ def tile_modalityadaptivemodule_pa_kernel(
                 for o in range(N_OUTPUTS):
                     project_one(0, o, 0)
                     store_row(0, o, 0)
-                invert(3)
-                normalise(3)
+                aggregate(4)
+                deviation(4)
                 project_one(0, 0, 1)
                 store_row(0, 0, 1)
+                invert(3)
                 quantise(1)
+                normalise(3)
                 for o in (1, 2):
                     project_one(0, o, 1)
                     store_row(0, o, 1)
@@ -498,10 +497,11 @@ def tile_modalityadaptivemodule_pa_kernel(
             store(u, 0)
             project(u, 1)
             store(u, 1)
+            if u + 3 < N_UNITS:
+                invert(u + 3)
             if u + 1 < N_UNITS:
                 quantise(u + 1)
             if u + 3 < N_UNITS:
-                invert(u + 3)
                 normalise(u + 3)
             project(u, 2)
             store(u, 2)

@@ -42,7 +42,8 @@ BN_AGGR_DIM = 2
 VECTOR_PAD = 16
 
 GROUPED_ON_GPSIMD = (2, 3, 4)
-SCALAR_ROWS = (((5, 0),), ((5, 1), (6, 0)), ((6, 1),), ((7, 0), (7, 1)), (), (), (), ())
+SCALAR_MEANS = (((5, 0),), ((5, 1), (6, 0)), ((6, 1), (7, 0)), ((7, 1),), (), (), (), ())
+SCALAR_ROWS = ((), ((5, 0), (5, 1)), ((6, 0), (6, 1)), ((7, 0), (7, 1)), (), (), (), ())
 LOADS_PER_STORE = 2
 NO_SUMS = ()
 ONE_SUM = ((1, 1),)
@@ -175,11 +176,13 @@ def tile_modalityadaptivemodule_pa_kernel(
         issue(weight_loads(1))
         issue(weight_loads(2))
         load_rows(3, 0, ROWS_PER_PARTITION)
+        load_words(3)
+        load_words(4)
         later_loads = [(load_vector, 1, i) for i in range(2)]
         for w in WEIGHTS_FIRST_USED_BY[1]:
             later_loads.append((load_bias, w))
         for w in WEIGHTS_FIRST_USED_BY[1]:
-            later_loads += weight_loads(w)
+            later_loads += weight_loads(w)[:4]
 
         def prepare_gain_shift(s):
             nc.scalar.copy(out=gain_shift[:, s, :, :], in_=gain_shift_bf[:, s, :, 0:PACK])
@@ -260,17 +263,23 @@ def tile_modalityadaptivemodule_pa_kernel(
         def invert(u):
             nc.vector.reciprocal(out=rstd[:, u, :], in_=std[:, u, :])
 
-        def normalise(u, engines=(nc.gpsimd, nc.gpsimd)):
+        def normalise_row(u, jj, engine):
             b, j0 = unit_place(u)
+            engine.tensor_scalar(
+                out=xhat_of[u][:, jj, :, :],
+                in0=x_sb[b][:, j0 + jj, :].rearrange("p (q t) -> p t q", t=PACK),
+                scalar1=neg_mean[:, u, jj : jj + 1], scalar2=rstd[:, u, jj : jj + 1],
+                op0=ALU.add, op1=ALU.mult,
+            )
+
+        def new_xhat(u):
             xhat = xhat_pool.tile([P, UNIT_J, PACK, P], F32)
-            for jj in range(UNIT_J):
-                engines[jj].tensor_scalar(
-                    out=xhat[:, jj, :, :],
-                    in0=x_sb[b][:, j0 + jj, :].rearrange("p (q t) -> p t q", t=PACK),
-                    scalar1=neg_mean[:, u, jj : jj + 1], scalar2=rstd[:, u, jj : jj + 1],
-                    op0=ALU.add, op1=ALU.mult,
-                )
             xhat_of[u] = xhat
+
+        def normalise(u):
+            new_xhat(u)
+            for jj in range(UNIT_J):
+                normalise_row(u, jj, nc.gpsimd)
 
         def transpose(u):
             xhat = xhat_of[u]
@@ -427,34 +436,39 @@ def tile_modalityadaptivemodule_pa_kernel(
         mean_on_scalar(1, 1)
         row_statistics(2, 0)
         invert(0)
-        normalise(0, (nc.vector, nc.vector))
+        new_xhat(0)
+        normalise_row(0, 0, nc.vector)
+        normalise_row(0, 1, nc.gpsimd)
         squares_on_scalar(1, 0)
         squares_on_scalar(1, 1)
         prepare_gain_shift(0)
         deviation(1)
         row_statistics(2, 1)
+        row_statistics(3, 0)
         aggregate(2)
         invert(1)
-        normalise(1)
+        new_xhat(1)
+        normalise_row(1, 0, nc.gpsimd)
         xt_rows = [transpose_row(0, jj) for jj in range(UNIT_J)]
         new_tn(0)
         new_operand(0)
         scale_shift_row(0, 0, xt_rows[0])
-        deviation(2)
         scale_shift_row(0, 1, xt_rows[1])
-        row_statistics(3, 0)
         row_statistics(3, 1)
         row_statistics(4, 0)
-        aggregate(3)
+        normalise_row(1, 1, nc.vector)
         for jj in range(UNIT_J):
             group_row(0, jj)
+        aggregate(3)
         for jj in range(UNIT_J):
             quantise_row(0, jj)
+        bias_accs = [spread_bias(w, acc_psum) for w in WEIGHTS_FIRST_USED_BY[0]]
+        keep_bias(0, bias_accs[0])
+        deviation(2)
+        keep_bias(1, bias_accs[1])
         invert(2)
         normalise(2)
-        bias_accs = [spread_bias(w, acc_psum) for w in WEIGHTS_FIRST_USED_BY[0]]
-        for w in WEIGHTS_FIRST_USED_BY[0]:
-            keep_bias(w, bias_accs[w])
+        keep_bias(2, bias_accs[2])
         row_statistics(4, 1)
         transpose(1)
         scale_shift(1)
@@ -466,6 +480,8 @@ def tile_modalityadaptivemodule_pa_kernel(
                 scalar_sum_pass(u, *place)
             if 0 < u < N_UNITS - 1:
                 scale_shift(u + 1)
+            for row in SCALAR_MEANS[u]:
+                mean_on_scalar(*row)
             for place in SCALAR_SUMS[u]:
                 scalar_sum(u, *place)
             if 0 < u < N_UNITS - 1:
@@ -476,7 +492,7 @@ def tile_modalityadaptivemodule_pa_kernel(
             if 4 < u + 3 < N_UNITS:
                 deviation(u + 3)
             for row in SCALAR_ROWS[u]:
-                statistics_on_scalar(*row)
+                squares_on_scalar(*row)
             if u == 0:
                 for o in range(N_OUTPUTS):
                     project_one(0, o, 0)
@@ -506,8 +522,8 @@ def tile_modalityadaptivemodule_pa_kernel(
             project(u, 2)
             store(u, 2)
             if u + 2 < N_UNITS:
-                if u in (1, 2):
-                    w = WEIGHTS_FIRST_USED_BY[1][u - 1]
+                if u in (2, 3):
+                    w = WEIGHTS_FIRST_USED_BY[1][u - 2]
                     keep_bias(w, spread_bias(w, scalar_psum))
                 if u + 2 == UNITS_PER_STREAM:
                     prepare_gain_shift(1)

@@ -92,7 +92,7 @@ def tile_modalityadaptivemodule_pa_kernel(
         gain_shift_bf = keep.tile([P, 2, 2, VECTOR_PAD], BF16)
         gain_shift = keep.tile([P, 2, 2, PACK], F32)
         bias_rows = keep.tile([P, N_OUT], BF16)
-        bias_all = keep.tile([P, N_WEIGHTS, N_OUT], F32)
+        bias_all = keep.tile([P, N_WEIGHTS, N_OUT], BF16)
         ident = keep.tile([P, P], F32)
         std = keep.tile([P, N_UNITS, UNIT_J], F32)
         one = keep.tile([P, 1], F32)
@@ -167,9 +167,9 @@ def tile_modalityadaptivemodule_pa_kernel(
         load_rows(0, 0, 1)
         load_rows(0, 1, UNIT_J)
         load_rows(0, UNIT_J, ROWS_PER_PARTITION)
+        issue([(load_vector, 0, i) for i in range(2)])
         load_rows(1, 0, UNIT_J)
         load_rows(1, UNIT_J, ROWS_PER_PARTITION)
-        issue([(load_vector, 0, i) for i in range(2)])
         issue([(load_bias, w) for w in WEIGHTS_FIRST_USED_BY[0]])
         load_rows(2, 0, ROWS_PER_PARTITION)
         issue(weight_loads(0))
@@ -188,7 +188,7 @@ def tile_modalityadaptivemodule_pa_kernel(
             nc.scalar.copy(out=gain_shift[:, s, :, :], in_=gain_shift_bf[:, s, :, 0:PACK])
 
         def spread_bias(w, pool):
-            acc = pool.tile([P, N_OUT], F32)
+            acc = pool.tile([P, N_OUT], BF16)
             nc.tensor.matmul(
                 out=acc[:], lhsT=select[:, w : w + 1].to_broadcast([P, P]), rhs=bias_rows[:],
                 start=True, stop=True,
@@ -259,6 +259,21 @@ def tile_modalityadaptivemodule_pa_kernel(
                             out=std[:, u, jj : jj + 1], in_=sum_squares[:, u, jj : jj + 1], func=ACT.Sqrt,
                             scale=1.0 / K, bias=EPS,
                         )
+
+        def deviation_row(u, jj):
+            if (u, jj) in by_vector:
+                nc.scalar.activation(
+                    out=std[:, u, jj : jj + 1], in_=mean_var[:, u, jj, 1:2], func=ACT.Sqrt, bias=EPS
+                )
+                nc.scalar.mul(out=neg_mean[:, u, jj : jj + 1], in_=mean_var[:, u, jj, 0:1], mul=-1.0)
+            else:
+                nc.scalar.activation(
+                    out=std[:, u, jj : jj + 1], in_=sum_squares[:, u, jj : jj + 1], func=ACT.Sqrt,
+                    scale=1.0 / K, bias=EPS,
+                )
+
+        def invert_row(u, jj):
+            nc.vector.reciprocal(out=rstd[:, u, jj : jj + 1], in_=std[:, u, jj : jj + 1])
 
         def invert(u):
             nc.vector.reciprocal(out=rstd[:, u, :], in_=std[:, u, :])
@@ -428,23 +443,26 @@ def tile_modalityadaptivemodule_pa_kernel(
             issue(later_loads[:LOADS_PER_STORE])
             later_loads[:] = later_loads[LOADS_PER_STORE:]
 
-        mean_on_scalar(1, 0)
+        mean_on_scalar(0, 1)
         row_statistics(0, 0)
-        row_statistics(0, 1)
-        aggregate(0)
-        deviation(0)
-        mean_on_scalar(1, 1)
+        aggregate_row(0, 0)
+        deviation_row(0, 0)
+        row_statistics(1, 0)
+        squares_on_scalar(0, 1)
+        invert_row(0, 0)
         row_statistics(2, 0)
-        invert(0)
         new_xhat(0)
         normalise_row(0, 0, nc.vector)
+        mean_on_scalar(1, 1)
+        deviation_row(0, 1)
+        invert_row(0, 1)
+        aggregate_row(1, 0)
         normalise_row(0, 1, nc.gpsimd)
-        squares_on_scalar(1, 0)
-        squares_on_scalar(1, 1)
         prepare_gain_shift(0)
-        deviation(1)
+        squares_on_scalar(1, 1)
         row_statistics(2, 1)
         row_statistics(3, 0)
+        deviation(1)
         aggregate(2)
         invert(1)
         new_xhat(1)

from contextlib import ExitStack

import concourse.mybir as mybir
from concourse.masks import make_identity

F32 = mybir.dt.float32
BF16 = mybir.dt.bfloat16
I32 = mybir.dt.int32
U32 = mybir.dt.uint32
U8 = mybir.dt.uint8
FP8X4 = mybir.dt.float8_e4m3fn_x4
ACT = mybir.ActivationFunctionType
ALU = mybir.AluOpType

P = 128
PACK = 4
K = P * PACK
N_OUT = 512
EPS = 1e-5

BLOCK_ROWS = 512
ROWS_PER_PARTITION = BLOCK_ROWS // P
N_BLOCKS = 4
BLOCKS_PER_STREAM = 2
UNIT_J = 2
UNITS_PER_BLOCK = ROWS_PER_PARTITION // UNIT_J
UNIT_ROWS = UNIT_J * P
N_UNITS = N_BLOCKS * UNITS_PER_BLOCK
UNITS_PER_STREAM = BLOCKS_PER_STREAM * UNITS_PER_BLOCK

N_OUTPUTS = 3
N_WEIGHTS = 5
WEIGHTS_USED_BY = ((0, 1, 2), (0, 3, 4))
WEIGHTS_FIRST_USED_BY = ((0, 1, 2), (3, 4))
SCALE_ROWS = K // 32
QUADRANT = 32

SELECT_COLUMNS = 16

BN_STATS_DIM = 6
BN_AGGR_DIM = 2
VECTOR_PAD = 16

GROUPED_ON_GPSIMD = (2, 3, 4)
SCALAR_MEANS = (((5, 0),), ((5, 1), (6, 0)), ((6, 1), (7, 0)), ((7, 1),), (), (), (), ())
SCALAR_ROWS = ((), ((5, 0), (5, 1)), ((6, 0), (6, 1)), ((7, 0), (7, 1)), (), (), (), ())
LOADS_PER_STORE = 2
NO_SUMS = ()
ONE_SUM = ((1, 1),)
TWO_SUMS = ((1, 1), (2, 1))
SCALAR_SUMS = (NO_SUMS, NO_SUMS, NO_SUMS, NO_SUMS, NO_SUMS, ONE_SUM, ONE_SUM, NO_SUMS)

FLOPS = 2 * N_BLOCKS * BLOCK_ROWS * K * 3 * N_OUT


def tile_modalityadaptivemodule_pa_kernel(
    tc,
    text, img, ln_t_g, ln_t_b, ln_i_g, ln_i_b,
    Wq_words, Wq_scales, bq,
    Wkt_words, Wkt_scales, bkt,
    Wvt_words, Wvt_scales, bvt,
    Wki_words, Wki_scales, bki,
    Wvi_words, Wvi_scales, bvi,
    out_0, out_1, out_2,
):
    nc = tc.nc
    streams = (text, img)
    gains_shifts = ((ln_t_g, ln_t_b), (ln_i_g, ln_i_b))
    weight_words = (Wq_words, Wkt_words, Wvt_words, Wki_words, Wvi_words)
    weight_scales = (Wq_scales, Wkt_scales, Wvt_scales, Wki_scales, Wvi_scales)
    biases = (bq, bkt, bvt, bki, bvi)
    outs = (out_0, out_1, out_2)

    with ExitStack() as ctx:
        keep = ctx.enter_context(tc.tile_pool(name="keep", bufs=1))
        xhat_pool = ctx.enter_context(tc.tile_pool(name="xhat_pool", bufs=N_UNITS))
        tn_pool = ctx.enter_context(tc.tile_pool(name="tn_pool", bufs=2))
        operand_pool = ctx.enter_context(tc.tile_pool(name="operand_pool", bufs=3))
        result_pool = ctx.enter_context(tc.tile_pool(name="result_pool", bufs=8))
        unread_pool = ctx.enter_context(tc.tile_pool(name="unread_pool", bufs=4))
        xt_psum = ctx.enter_context(tc.psum_pool(name="xt_psum", bufs=3))
        acc_psum = ctx.enter_context(tc.psum_pool(name="acc_psum", bufs=4))
        scalar_psum = ctx.enter_context(tc.psum_pool(name="scalar_psum", bufs=1))
        ctx.enter_context(tc.manual_schedule())

        x_sb = [
            keep.tile([P, ROWS_PER_PARTITION, K], BF16, name="x%d" % b)
            for b in range(N_BLOCKS)
        ]
        w_words = keep.tile([P, N_WEIGHTS, N_OUT], U32, align_bytes=64)
        w_scales = keep.tile([P, N_WEIGHTS, N_OUT], U8, align_bytes=64)
        gain_shift_bf = keep.tile([P, 2, 2, VECTOR_PAD], BF16)
        gain_shift = keep.tile([P, 2, 2, PACK], F32)
        bias_rows = keep.tile([P, N_OUT], BF16)
        bias_all = keep.tile([P, N_WEIGHTS, N_OUT], BF16)
        ident = keep.tile([P, P], F32)
        std = keep.tile([P, N_UNITS, UNIT_J], F32)
        one = keep.tile([P, 1], F32)
        unread_root = keep.tile([P, 1], F32)
        select = keep.tile([P, SELECT_COLUMNS], BF16)
        stats = keep.tile([P, N_UNITS, UNIT_J, BN_STATS_DIM], F32)
        mean_var = keep.tile([P, N_UNITS, UNIT_J, BN_AGGR_DIM], F32)
        neg_mean = keep.tile([P, N_UNITS, UNIT_J], F32)
        sum_squares = keep.tile([P, N_UNITS, UNIT_J], F32)
        rstd = keep.tile([P, N_UNITS, UNIT_J], F32)

        by_vector = set()
        xhat_of = {}
        xt_of = {}
        planes_of = {}
        grouped_of = {}
        operand_of = {}
        result_of = {}
        scalar_acc_of = {}

        def block_view(dram, b):
            return dram[b].rearrange("(p j) c -> p j c", j=ROWS_PER_PARTITION)

        def unit_place(u):
            b, half = divmod(u, UNITS_PER_BLOCK)
            return b, half * UNIT_J

        def load_rows(b, j0, j1):
            source = block_view(streams[b // BLOCKS_PER_STREAM], b % BLOCKS_PER_STREAM)
            nc.sync.dma_start(out=x_sb[b][:, j0:j1, :], in_=source[:, j0:j1, :])

        def load_bias(w):
            nc.sync.dma_start(
                out=bias_rows[w : w + 1, :], in_=biases[w].rearrange("(o n) -> o n", o=1)
            )

        def load_vector(s, i):
            with nc.allow_non_contiguous_dma(reason="four bfloat16 values to a partition"):
                nc.sync.dma_start(
                    out=gain_shift_bf[:, s, i, 0:PACK],
                    in_=gains_shifts[s][i].rearrange("(p t) -> p t", t=PACK),
                )

        def load_scales(w, quad):
            nc.sync.dma_start(
                out=w_scales[QUADRANT * quad : QUADRANT * quad + PACK, w, :].bitcast(I32),
                in_=weight_scales[w][0, PACK * quad : PACK * (quad + 1), :].bitcast(I32),
            )

        def load_words(w):
            nc.sync.dma_start(
                out=w_words[:, w, :].bitcast(I32),
                in_=weight_words[w][0].rearrange("p n t -> p (n t)").bitcast(I32),
            )

        def weight_loads(w):
            quads = SCALE_ROWS // PACK
            return [(load_scales, w, quad) for quad in range(quads)] + [(load_words, w)]

        def issue(loads):
            for load, *what in loads:
                load(*what)

        nc.gpsimd.memset(one[:], 1.0)
        nc.gpsimd.memset(bias_rows[:].bitcast(I32), 0)
        nc.gpsimd.memset(w_scales[:].bitcast(I32), 0)
        make_identity(nc, ident[:])
        nc.gpsimd.tensor_copy(out=select[:], in_=ident[:, 0:SELECT_COLUMNS])

        nc.scalar.activation(out=unread_root[:], in_=one[:], func=ACT.Sqrt)

        load_rows(0, 0, 1)
        load_rows(0, 1, UNIT_J)
        load_rows(0, UNIT_J, ROWS_PER_PARTITION)
        issue([(load_vector, 0, i) for i in range(2)])
        load_rows(1, 0, UNIT_J)
        load_rows(1, UNIT_J, ROWS_PER_PARTITION)
        issue([(load_bias, w) for w in WEIGHTS_FIRST_USED_BY[0]])
        load_rows(2, 0, ROWS_PER_PARTITION)
        issue(weight_loads(0))
        issue(weight_loads(1))
        issue(weight_loads(2))
        load_rows(3, 0, ROWS_PER_PARTITION)
        load_words(3)
        load_words(4)
        later_loads = [(load_vector, 1, i) for i in range(2)]
        for w in WEIGHTS_FIRST_USED_BY[1]:
            later_loads.append((load_bias, w))
        for w in WEIGHTS_FIRST_USED_BY[1]:
            later_loads += weight_loads(w)[:4]

        def prepare_gain_shift(s):
            nc.scalar.copy(out=gain_shift[:, s, :, :], in_=gain_shift_bf[:, s, :, 0:PACK])

        def spread_bias(w, pool):
            acc = pool.tile([P, N_OUT], BF16)
            nc.tensor.matmul(
                out=acc[:], lhsT=select[:, w : w + 1].to_broadcast([P, P]), rhs=bias_rows[:],
                start=True, stop=True,
            )
            return acc

        def keep_bias(w, acc):
            nc.scalar.copy(out=bias_all[:, w, :], in_=acc[:])

        def row_statistics(u, jj):
            b, j0 = unit_place(u)
            nc.vector.bn_stats(out=stats[:, u, jj, :], in_=x_sb[b][:, j0 + jj, :])

        def aggregate_row(u, jj):
            nc.vector.bn_aggr(out=mean_var[:, u, jj, :], in_=stats[:, u, jj, :])
            by_vector.add((u, jj))

        def aggregate(u):
            for jj in range(UNIT_J):
                aggregate_row(u, jj)

        def statistics(u):
            for jj in range(UNIT_J):
                row_statistics(u, jj)
            aggregate(u)

        def mean_on_scalar(u, jj):
            b, j0 = unit_place(u)
            scaled = unread_pool.tile([P, K], BF16)
            nc.scalar.activation(
                out=scaled[:], in_=x_sb[b][:, j0 + jj, :], func=ACT.Identity,
                scale=-1.0 / K, accum_out=neg_mean[:, u, jj : jj + 1],
            )

        def squares_on_scalar(u, jj):
            b, j0 = unit_place(u)
            squares = unread_pool.tile([P, K], BF16)
            nc.scalar.activation(
                out=squares[:], in_=x_sb[b][:, j0 + jj, :], func=ACT.Square,
                bias=neg_mean[:, u, jj : jj + 1], accum_out=sum_squares[:, u, jj : jj + 1],
            )

        def statistics_on_scalar(u, jj):
            mean_on_scalar(u, jj)
            squares_on_scalar(u, jj)

        def deviation(u):
            kinds = [(u, jj) in by_vector for jj in range(UNIT_J)]
            if all(kinds):
                nc.scalar.activation(
                    out=std[:, u, :], in_=mean_var[:, u, :, 1], func=ACT.Sqrt, bias=EPS
                )
                nc.scalar.mul(out=neg_mean[:, u, :], in_=mean_var[:, u, :, 0], mul=-1.0)
            elif not any(kinds):
                nc.scalar.activation(
                    out=std[:, u, :], in_=sum_squares[:, u, :], func=ACT.Sqrt,
                    scale=1.0 / K, bias=EPS,
                )
            else:
                for jj in range(UNIT_J):
                    if kinds[jj]:
                        nc.scalar.activation(
                            out=std[:, u, jj : jj + 1], in_=mean_var[:, u, jj, 1:2], func=ACT.Sqrt, bias=EPS
                        )
                        nc.scalar.mul(out=neg_mean[:, u, jj : jj + 1], in_=mean_var[:, u, jj, 0:1], mul=-1.0)
                    else:
                        nc.scalar.activation(
                            out=std[:, u, jj : jj + 1], in_=sum_squares[:, u, jj : jj + 1], func=ACT.Sqrt,
                            scale=1.0 / K, bias=EPS,
                        )

        def deviation_row(u, jj):
            if (u, jj) in by_vector:
                nc.scalar.activation(
                    out=std[:, u, jj : jj + 1], in_=mean_var[:, u, jj, 1:2], func=ACT.Sqrt, bias=EPS
                )
                nc.scalar.mul(out=neg_mean[:, u, jj : jj + 1], in_=mean_var[:, u, jj, 0:1], mul=-1.0)
            else:
                nc.scalar.activation(
                    out=std[:, u, jj : jj + 1], in_=sum_squares[:, u, jj : jj + 1], func=ACT.Sqrt,
                    scale=1.0 / K, bias=EPS,
                )

        def invert_row(u, jj):
            nc.vector.reciprocal(out=rstd[:, u, jj : jj + 1], in_=std[:, u, jj : jj + 1])

        def invert(u):
            nc.vector.reciprocal(out=rstd[:, u, :], in_=std[:, u, :])

        def normalise_row(u, jj, engine):
            b, j0 = unit_place(u)
            engine.tensor_scalar(
                out=xhat_of[u][:, jj, :, :],
                in0=x_sb[b][:, j0 + jj, :].rearrange("p (q t) -> p t q", t=PACK),
                scalar1=neg_mean[:, u, jj : jj + 1], scalar2=rstd[:, u, jj : jj + 1],
                op0=ALU.add, op1=ALU.mult,
            )

        def new_xhat(u):
            xhat = xhat_pool.tile([P, UNIT_J, PACK, P], F32)
            xhat_of[u] = xhat

        def normalise(u):
            new_xhat(u)
            for jj in range(UNIT_J):
                normalise_row(u, jj, nc.gpsimd)

        def transpose(u):
            xhat = xhat_of[u]
            xt_of[u] = []
            for half in range(2):
                xt = xt_psum.tile([P, 2, UNIT_ROWS], F32)
                xt_of[u] += [xt[:, 0, :], xt[:, 1, :]]
            for jj in range(UNIT_J):
                for t in range(PACK):
                    nc.tensor.transpose(
                        out=xt_of[u][t][:, jj * P : (jj + 1) * P],
                        in_=xhat[:, jj, t, :],
                        identity=ident[:],
                    )

        def new_tn(u):
            planes = tn_pool.tile([P, PACK, UNIT_ROWS], BF16)
            planes_of[u] = planes
            grouped = tn_pool.tile([P, UNIT_ROWS, PACK], BF16, align_bytes=64)
            grouped_of[u] = grouped

        def transpose_row(u, jj):
            xt = xt_psum.tile([P, PACK, P], F32)
            for t in range(PACK):
                nc.tensor.transpose(
                    out=xt[:, t, :], in_=xhat_of[u][:, jj, t, :], identity=ident[:]
                )
            return xt

        def scale_shift_plane(u, t, source, columns):
            s = u // UNITS_PER_STREAM
            nc.scalar.activation(
                out=planes_of[u][:, t, columns], in_=source, func=ACT.Identity,
                scale=gain_shift[:, s, 0, t : t + 1], bias=gain_shift[:, s, 1, t : t + 1],
            )

        def scale_shift_row(u, jj, xt):
            for t in range(PACK):
                scale_shift_plane(u, t, xt[:, t, :], slice(jj * P, (jj + 1) * P))

        def group_on_gpsimd(u):
            nc.gpsimd.tensor_scalar(
                out=grouped_of[u][:], in0=planes_of[u][:].rearrange("p t c -> p c t"),
                scalar1=1.0, scalar2=0.0, op0=ALU.mult, op1=ALU.add,
            )

        def group(u, copy=nc.scalar.copy):
            copy(
                out=grouped_of[u][:].rearrange("p (c i) t -> p c t i", i=4),
                in_=planes_of[u][:].rearrange("p t (c i) -> p c t i", i=4),
            )

        def scale_shift(u):
            new_tn(u)
            for t in range(PACK):
                scale_shift_plane(u, t, xt_of[u][t], slice(0, UNIT_ROWS))

        def new_operand(u):
            codes = operand_pool.tile([P, UNIT_ROWS], U32, align_bytes=64)
            code_scales = operand_pool.tile([P, UNIT_ROWS], U8, align_bytes=64)
            operand_of[u] = (codes, code_scales)

        def quantise_columns(u, columns):
            codes, code_scales = operand_of[u]
            nc.vector.quantize_mx(
                out=codes[:, columns].bitcast(FP8X4),
                scales=code_scales[:, columns],
                in_=grouped_of[u][:, columns, :].rearrange("p c t -> p (c t)"),
            )

        def group_row(u, jj):
            columns = slice(jj * P, (jj + 1) * P)
            nc.vector.tensor_copy(
                out=grouped_of[u][:, columns, :].rearrange("p (c i) t -> p c t i", i=4),
                in_=planes_of[u][:, :, columns].rearrange("p t (c i) -> p c t i", i=4),
            )

        def quantise_row(u, jj):
            quantise_columns(u, slice(jj * P, (jj + 1) * P))

        def quantise(u):
            new_operand(u)
            quantise_columns(u, slice(0, UNIT_ROWS))

        def multiply(u, o, jj, acc):
            codes, code_scales = operand_of[u]
            w = WEIGHTS_USED_BY[u // UNITS_PER_STREAM][o]
            rows = slice(jj * P, (jj + 1) * P)
            nc.tensor.matmul_mx(
                out=acc[:],
                lhsT=codes[:, rows].bitcast(FP8X4),
                lhsT_scale=code_scales[:, rows],
                rhs=w_words[:, w, :].bitcast(FP8X4),
                rhs_scale=w_scales[:, w, :],
                start=True,
                stop=True,
            )

        def bias_of(u, o):
            return bias_all[:, WEIGHTS_USED_BY[u // UNITS_PER_STREAM][o], :]

        def new_results(u):
            for o in range(N_OUTPUTS):
                result = result_pool.tile([P, UNIT_J, N_OUT], F32)
                result_of[u, o] = result

        def scalar_sum_pass(u, o, jj):
            acc = scalar_psum.tile([P, N_OUT], F32)
            multiply(u, o, jj, acc)
            scalar_acc_of[u, o, jj] = acc

        def scalar_sum(u, o, jj):
            place = result_of[u, o][:, jj, :]
            nc.scalar.copy(out=place, in_=scalar_acc_of[u, o, jj][:])
            nc.gpsimd.tensor_tensor(out=place, in0=place, in1=bias_of(u, o), op=ALU.add)

        def project(u, o):
            for jj in range(UNIT_J):
                if (o, jj) not in SCALAR_SUMS[u]:
                    acc = acc_psum.tile([P, N_OUT], F32)
                    multiply(u, o, jj, acc)
                    nc.vector.tensor_tensor(
                        out=result_of[u, o][:, jj, :], in0=acc[:], in1=bias_of(u, o), op=ALU.add
                    )

        def project_one(u, o, jj):
            acc = acc_psum.tile([P, N_OUT], F32)
            multiply(u, o, jj, acc)
            nc.vector.tensor_tensor(
                out=result_of[u, o][:, jj, :], in0=acc[:], in1=bias_of(u, o), op=ALU.add
            )

        def store_row(u, o, jj):
            b, j0 = unit_place(u)
            nc.sync.dma_start(
                out=block_view(outs[o], b)[:, j0 + jj, :], in_=result_of[u, o][:, jj, :]
            )
            issue(later_loads[:1])
            later_loads[:] = later_loads[1:]

        def store(u, o):
            b, j0 = unit_place(u)
            nc.sync.dma_start(
                out=block_view(outs[o], b)[:, j0 : j0 + UNIT_J, :], in_=result_of[u, o][:]
            )
            issue(later_loads[:LOADS_PER_STORE])
            later_loads[:] = later_loads[LOADS_PER_STORE:]

        mean_on_scalar(0, 1)
        row_statistics(0, 0)
        aggregate_row(0, 0)
        deviation_row(0, 0)
        row_statistics(1, 0)
        squares_on_scalar(0, 1)
        invert_row(0, 0)
        row_statistics(2, 0)
        new_xhat(0)
        normalise_row(0, 0, nc.vector)
        mean_on_scalar(1, 1)
        deviation_row(0, 1)
        invert_row(0, 1)
        aggregate_row(1, 0)
        normalise_row(0, 1, nc.gpsimd)
        prepare_gain_shift(0)
        squares_on_scalar(1, 1)
        row_statistics(2, 1)
        row_statistics(3, 0)
        deviation(1)
        aggregate(2)
        invert(1)
        new_xhat(1)
        normalise_row(1, 0, nc.gpsimd)
        xt_rows = [transpose_row(0, jj) for jj in range(UNIT_J)]
        new_tn(0)
        new_operand(0)
        scale_shift_row(0, 0, xt_rows[0])
        scale_shift_row(0, 1, xt_rows[1])
        row_statistics(3, 1)
        row_statistics(4, 0)
        normalise_row(1, 1, nc.vector)
        for jj in range(UNIT_J):
            group_row(0, jj)
        aggregate(3)
        for jj in range(UNIT_J):
            quantise_row(0, jj)
        bias_accs = [spread_bias(w, acc_psum) for w in WEIGHTS_FIRST_USED_BY[0]]
        keep_bias(0, bias_accs[0])
        deviation(2)
        keep_bias(1, bias_accs[1])
        invert(2)
        normalise(2)
        keep_bias(2, bias_accs[2])
        row_statistics(4, 1)
        transpose(1)
        scale_shift(1)
        group(1)
        deviation(3)
        for u in range(N_UNITS):
            new_results(u)
            for place in SCALAR_SUMS[u]:
                scalar_sum_pass(u, *place)
            if 0 < u < N_UNITS - 1:
                scale_shift(u + 1)
            for row in SCALAR_MEANS[u]:
                mean_on_scalar(*row)
            for place in SCALAR_SUMS[u]:
                scalar_sum(u, *place)
            if 0 < u < N_UNITS - 1:
                if u + 1 in GROUPED_ON_GPSIMD:
                    group_on_gpsimd(u + 1)
                else:
                    group(u + 1)
            if 4 < u + 3 < N_UNITS:
                deviation(u + 3)
            for row in SCALAR_ROWS[u]:
                squares_on_scalar(*row)
            if u == 0:
                for o in range(N_OUTPUTS):
                    project_one(0, o, 0)
                    store_row(0, o, 0)
                aggregate(4)
                deviation(4)
                project_one(0, 0, 1)
                store_row(0, 0, 1)
                invert(3)
                quantise(1)
                normalise(3)
                for o in (1, 2):
                    project_one(0, o, 1)
                    store_row(0, o, 1)
                transpose(2)
                continue
            project(u, 0)
            store(u, 0)
            project(u, 1)
            store(u, 1)
            if u + 3 < N_UNITS:
                invert(u + 3)
            if u + 1 < N_UNITS:
                quantise(u + 1)
            if u + 3 < N_UNITS:
                normalise(u + 3)
            project(u, 2)
            store(u, 2)
            if u + 2 < N_UNITS:
                if u in (2, 3):
                    w = WEIGHTS_FIRST_USED_BY[1][u - 2]
                    keep_bias(w, spread_bias(w, scalar_psum))
                if u + 2 == UNITS_PER_STREAM:
                    prepare_gain_shift(1)
                transpose(u + 2)
